import numpy as np
import ml_dtypes


def mxq(x, axis, fmt="e4m3"):
    dtype, down = {"e4m3": (ml_dtypes.float8_e4m3fn, 7), "e5m2": (ml_dtypes.float8_e5m2, 14)}[fmt]
    v = np.moveaxis(np.asarray(x, np.float32).astype(ml_dtypes.bfloat16).astype(np.float64), axis, -1)
    blocks = v.reshape(v.shape[:-1] + (-1, 32))
    amax = np.abs(blocks).max(-1, keepdims=True)
    byte = np.maximum(np.where(amax > 0, np.frexp(amax)[1] - 1 + 127, 0) - down, 1)
    scale = np.exp2(byte - 127.0)
    codes = (blocks / scale).astype(np.float32).astype(dtype).astype(np.float64)
    return np.moveaxis((codes * scale).reshape(v.shape), -1, axis)


WIDE = False


def mx_kscale(k):
    if not WIDE:
        return np.ones(k)
    levels = np.array([10, -10, 5, -5, 0])
    a = np.random.permutation(np.resize(levels, k // 512 * 4)).reshape(k // 512, 4)
    idx = np.arange(k)
    return np.exp2(a[idx // 512, idx % 128 // 32])


BF16 = ml_dtypes.bfloat16


def bf(x):
    return np.asarray(x, np.float32).astype(BF16)


def f64(x):
    return np.asarray(x).astype(np.float64)


B, C, H, W = 1, 1024, 32, 32
C2 = C // 2
N = H * W


def sigmoid(v):
    return 1.0 / (1.0 + np.exp(-v))


def setup_inputs():
    s = mx_kscale(C)
    amp = 0.4 + 1.2 * np.random.random((B, 1, H, W))
    return {
        'x1': bf(np.random.standard_normal((B, C, H, W)) * amp * s[None, :, None, None]),
        'wq1': bf(np.random.standard_normal((C2, C)) * 0.7 / np.sqrt(C) / s[None, :]),
        'bq1': bf(np.random.standard_normal(C2) * 0.3),
        'wv1': bf(np.random.standard_normal((C2, C)) * 6.0 / np.sqrt(N * C) / s[None, :]),
        'bv1': bf(np.random.standard_normal(C2) * 6.0 / N),
        'k2': bf(np.random.standard_normal((B, N)) * 0.8),
    }


def reference(x1, wq1, bq1, wv1, bv1, k2):
    xq = mxq(f64(x1).reshape(B, C, N), 1, 'e4m3')
    q1 = ((mxq(f64(wq1), 1, 'e4m3') @ xq) + f64(bq1)[None, :, None]).max(axis=1)
    v1 = (mxq(f64(wv1), 1, 'e4m3') @ xq) + f64(bv1)[None, :, None]
    att2 = 1.0 - sigmoid(q1[:, :, None] * f64(k2)[:, None, :])
    out = mxq(v1, 2, 'e4m3') @ mxq(att2, 2, 'e4m3').transpose(0, 2, 1)
    return out.reshape(B, C2, H, W)

@@ -1,0 +1,317 @@
+from contextlib import ExitStack
+
+import concourse.mybir as mybir
+from concourse.masks import make_identity
+
+F32 = mybir.dt.float32
+BF16 = mybir.dt.bfloat16
+U32 = mybir.dt.uint32
+U8 = mybir.dt.uint8
+FP8X4 = mybir.dt.float8_e4m3fn_x4
+ADD = mybir.AluOpType.add
+SUBTRACT = mybir.AluOpType.subtract
+MAX = mybir.AluOpType.max
+IDENTITY = mybir.ActivationFunctionType.Identity
+SIGMOID = mybir.ActivationFunctionType.Sigmoid
+
+P = 128
+PACK = 4
+K_PASS = P * PACK
+CHANNELS = 1024
+PIXELS = 1024
+OUT_CHANNELS = 512
+PASSES = 2
+HALF = 512
+HALVES = PIXELS // HALF
+TILES = OUT_CHANNELS // P
+PIECES = 3
+
+FLOPS = 3 * 2 * OUT_CHANNELS * CHANNELS * PIXELS
+
+
+def load_weight(nc, keep, weight, label):
+    rows = keep.tile([P, TILES * CHANNELS], BF16, name=label + "_rows")
+    by_tile = rows[:].rearrange("p (t c) -> p t c", t=TILES)
+    for first in range(0, TILES, 2):
+        nc.sync.dma_start(
+            out=by_tile[:, first : first + 2, :],
+            in_=weight[first * P : (first + 2) * P, :].rearrange("(t p) c -> p t c", p=P),
+        )
+    return rows
+
+
+def turn_weight(nc, keep, psum, rows, ident_f32, label):
+    words = rows[:].bitcast(F32)
+    grouped = keep.tile([P, PASSES * OUT_CHANNELS * PACK], BF16, name=label + "_grouped", align_bytes=64)
+    grouped_words = grouped[:].bitcast(F32).rearrange("p (g o u) -> p g o u", g=PASSES, u=2)
+    for t in range(TILES):
+        turned = psum.tile([P, PASSES * 2, P], F32, name=label + "_turned", tag="bank")
+        for b in range(PASSES * 2):
+            first_word = (t * PASSES * 2 + b) * P
+            nc.tensor.transpose(turned[:, b, :], words[:, first_word : first_word + P], ident_f32[:])
+        nc.scalar.copy(
+            out=grouped_words[:, :, t * P : (t + 1) * P, :],
+            in_=turned[:].rearrange("p (g u) o -> p g o u", u=2),
+        )
+    return grouped
+
+
+def quantise_weight(nc, keep, grouped, label):
+    codes = keep.tile([P, PASSES, OUT_CHANNELS], U32, name=label + "_codes", align_bytes=64)
+    scales = keep.tile([P, PASSES, OUT_CHANNELS], U8, name=label + "_scales", align_bytes=64)
+    nc.vector.quantize_mx(
+        out=codes[:].rearrange("p g o -> p (g o)").bitcast(FP8X4),
+        scales=scales[:].rearrange("p g o -> p (g o)"),
+        in_=grouped[:],
+    )
+    return codes, scales
+
+
+def quantise_columns(nc, grouped, codes, scales, g, columns):
+    nc.vector.quantize_mx(
+        out=codes[:, g, columns].bitcast(FP8X4),
+        scales=scales[:, g, columns],
+        in_=grouped[:, g, columns, :].rearrange("p n t -> p (n t)"),
+    )
+
+
+def tile_cross_module_pa_kernel(tc, x1, wq1, bq1, wv1, bv1, k2, out):
+    nc = tc.nc
+    x_rows = x1.rearrange("b c h w -> (b c) (h w)")
+    out_rows = out.rearrange("b c h w -> (b c) (h w)")
+
+    with ExitStack() as ctx:
+        keep = ctx.enter_context(tc.tile_pool(name="keep", bufs=1))
+        ring = ctx.enter_context(tc.tile_pool(name="ring", bufs=4))
+        psum = ctx.enter_context(tc.psum_pool(name="psum", bufs=8))
+        ctx.enter_context(tc.manual_schedule())
+
+        ident_f32 = keep.tile([P, P], F32)
+        make_identity(nc, ident_f32[:])
+        ident_bf16 = keep.tile([P, P], BF16)
+        make_identity(nc, ident_bf16[:])
+        ones = keep.tile([P, P], BF16)
+        nc.vector.memset(ones[:], 1.0)
+
+        bq_rows = keep.tile([P, P], BF16)
+        nc.vector.memset(bq_rows[:], 0.0)
+        nc.scalar.dma_start(out=bq_rows[0:TILES, :], in_=bq1.rearrange("(t p) -> t p", p=P))
+        bv_row = keep.tile([P, OUT_CHANNELS], BF16)
+        nc.vector.memset(bv_row[:], 0.0)
+        nc.scalar.dma_start(out=bv_row[0:1, :], in_=bv1.rearrange("(r c) -> r c", r=1))
+        k2_rows = keep.tile([P, PIXELS], BF16)
+        nc.vector.memset(k2_rows[:], 0.0)
+        for piece in range(PIECES):
+            nc.scalar.dma_start(out=k2_rows[piece : piece + 1, :], in_=k2)
+        q_pieces = keep.tile([P, HALVES * TILES, P], BF16)
+        nc.vector.memset(q_pieces[:], 0.0)
+
+        warm_in = keep.tile([P, 1], F32)
+        nc.vector.memset(warm_in[:], 0.0)
+        warm_out = keep.tile([P, 1], F32)
+        nc.scalar.activation(out=warm_out[:], in_=warm_in[:], func=SIGMOID)
+
+        wq_rows = load_weight(nc, keep, wq1, "wq")
+        x_sb = keep.tile([P, PASSES, PACK, PIXELS], BF16)
+        for g in range(PASSES):
+            for u in range(2):
+                first = g * K_PASS + u * 2 * P
+                nc.sync.dma_start(
+                    out=x_sb[:, g, 2 * u : 2 * u + 2, :],
+                    in_=x_rows[first : first + 2 * P, :].rearrange("(q e) n -> q e n", e=2),
+                )
+        wv_rows = load_weight(nc, keep, wv1, "wv")
+
+        x_grouped = keep.tile([P, PASSES, PIXELS, PACK], BF16, align_bytes=64)
+        x_codes = keep.tile([P, PASSES, PIXELS], U32, align_bytes=64)
+        x_scales = keep.tile([P, PASSES, PIXELS], U8, align_bytes=64)
+        att_grouped = keep.tile([P, PASSES, PIXELS, PACK], BF16, align_bytes=64)
+        att_codes = keep.tile([P, PASSES, PIXELS], U32, align_bytes=64)
+        att_scales = keep.tile([P, PASSES, PIXELS], U8, align_bytes=64)
+        v_grouped = keep.tile([P, PASSES, OUT_CHANNELS, PACK], BF16, align_bytes=64)
+        v_codes = keep.tile([P, PASSES, OUT_CHANNELS], U32, align_bytes=64)
+        v_scales = keep.tile([P, PASSES, OUT_CHANNELS], U8, align_bytes=64)
+        bq_cols = keep.tile([P, TILES], F32)
+        bv_all = keep.tile([P, OUT_CHANNELS], F32)
+        q_cols = keep.tile([P, HALVES * TILES], F32)
+        q_rest = keep.tile([P, HALVES * TILES], F32)
+        q_rows = keep.tile([P, PIXELS], BF16)
+
+        def half(h):
+            return slice(h * HALF, (h + 1) * HALF)
+
+        def block(t):
+            return slice(t * P, (t + 1) * P)
+
+        def spread_biases():
+            bq_turned = psum.tile([P, P], BF16, tag="bank")
+            nc.tensor.transpose(bq_turned[:], bq_rows[:], ident_bf16[:])
+            nc.scalar.copy(out=bq_cols[:], in_=bq_turned[:, 0:TILES])
+            bv_bank = psum.tile([P, OUT_CHANNELS], F32, tag="bank")
+            nc.tensor.matmul(out=bv_bank[:], lhsT=ones[:], rhs=bv_row[:], start=True, stop=True)
+            nc.scalar.copy(out=bv_all[:], in_=bv_bank[:])
+
+        def regroup_x(g):
+            for h in range(HALVES):
+                regrouped = x_grouped[:, g, half(h), :].rearrange("p (n i) t -> p n t i", i=4)
+                as_loaded = x_sb[:, g, :, half(h)].rearrange("p t (n i) -> p n t i", i=4)
+                if h == 0:
+                    nc.vector.tensor_copy(out=regrouped, in_=as_loaded)
+                else:
+                    nc.scalar.copy(out=regrouped, in_=as_loaded)
+
+        def quantise_x(g, h):
+            quantise_columns(nc, x_grouped, x_codes, x_scales, g, half(h))
+
+        def project_q(sums, h, g):
+            for t in range(TILES):
+                nc.tensor.matmul_mx(
+                    out=sums[t][:],
+                    lhsT=wq_codes[:, g, block(t)].bitcast(FP8X4),
+                    lhsT_scale=wq_scales[:, g, block(t)],
+                    rhs=x_codes[:, g, half(h)].bitcast(FP8X4),
+                    rhs_scale=x_scales[:, g, half(h)],
+                    start=(g == 0),
+                    stop=(g == PASSES - 1),
+                )
+
+        def four_banks(label):
+            banks = []
+            for t in range(TILES):
+                banks.append(psum.tile([P, HALF], F32, name=label, tag="bank"))
+            return banks
+
+        def tile_maximum(sums):
+            best = ring.tile([P, HALF], F32, name="best")
+            nc.scalar.activation(out=best[:], in_=sums[0][:], func=IDENTITY, bias=bq_cols[:, 0:1])
+            for t in range(1, TILES):
+                better = ring.tile([P, HALF], F32, name="best")
+                nc.vector.scalar_tensor_tensor(
+                    out=better[:], in0=sums[t][:], scalar=bq_cols[:, t : t + 1], in1=best[:], op0=ADD, op1=MAX
+                )
+                best = better
+            return best
+
+        def partition_maximum(best, h):
+            tiles = slice(h * TILES, (h + 1) * TILES)
+            best_turned = psum.tile([P, TILES, P], F32, tag="bank")
+            for t in range(TILES):
+                nc.tensor.transpose(best_turned[:, t, :], best[:, block(t)], ident_f32[:])
+            nc.vector.tensor_reduce(out=q_cols[:, tiles], in_=best_turned[:], axis=mybir.AxisListType.X, op=MAX)
+            nc.vector.tensor_copy(out=q_pieces[:, tiles, 0], in_=q_cols[:, tiles])
+            nc.vector.tensor_tensor(out=q_rest[:, tiles], in0=q_cols[:, tiles], in1=q_pieces[:, tiles, 0], op=SUBTRACT)
+            nc.vector.tensor_copy(out=q_pieces[:, tiles, 1], in_=q_rest[:, tiles])
+            nc.vector.tensor_tensor(out=q_pieces[:, tiles, 2], in0=q_rest[:, tiles], in1=q_pieces[:, tiles, 1], op=SUBTRACT)
+
+        def rows_of_q(h):
+            pieces_turned = psum.tile([P, TILES, P], BF16, tag="bank")
+            for t in range(TILES):
+                nc.tensor.transpose(pieces_turned[:, t, :], q_pieces[:, h * TILES + t, :], ident_bf16[:])
+            nc.scalar.copy(out=q_rows[:, half(h)], in_=pieces_turned[:].rearrange("p t n -> p (t n)"))
+
+        def attention_tile(g, m_tile):
+            product = psum.tile([P, PACK, P], F32, tag="bank")
+            for j in range(PACK):
+                nc.tensor.matmul(
+                    out=product[:, j, :],
+                    lhsT=k2_rows[:, block(g * PACK + j)],
+                    rhs=q_rows[:, block(m_tile)],
+                    start=True,
+                    stop=True,
+                )
+            nc.scalar.activation(
+                out=att_grouped[:, g, block(m_tile), :],
+                in_=product[:].rearrange("p j m -> p m j"),
+                func=SIGMOID,
+                scale=-1.0,
+            )
+
+        def value_tile(g, c_tile):
+            sums = psum.tile([P, PACK, P], F32, name="v_sums", tag="bank")
+            for j in range(PACK):
+                for gc in range(PASSES):
+                    nc.tensor.matmul_mx(
+                        out=sums[:, j, :],
+                        lhsT=x_codes[:, gc, block(g * PACK + j)].bitcast(FP8X4),
+                        lhsT_scale=x_scales[:, gc, block(g * PACK + j)],
+                        rhs=wv_codes[:, gc, block(c_tile)].bitcast(FP8X4),
+                        rhs_scale=wv_scales[:, gc, block(c_tile)],
+                        start=(gc == 0),
+                        stop=(gc == PASSES - 1),
+                    )
+            nc.vector.tensor_tensor(
+                out=v_grouped[:, g, block(c_tile), :],
+                in0=sums[:].rearrange("p j c -> p c j"),
+                in1=bv_all[:, block(c_tile)].unsqueeze(2).to_broadcast([P, P, PACK]),
+                op=ADD,
+            )
+
+        def output_pass(sums, h, c_tile, g):
+            nc.tensor.matmul_mx(
+                out=sums[:],
+                lhsT=v_codes[:, g, block(c_tile)].bitcast(FP8X4),
+                lhsT_scale=v_scales[:, g, block(c_tile)],
+                rhs=att_codes[:, g, half(h)].bitcast(FP8X4),
+                rhs_scale=att_scales[:, g, half(h)],
+                start=(g == 0),
+                stop=(g == PASSES - 1),
+            )
+
+        def store_output(sums, h, c_tile):
+            result = ring.tile([P, HALF], F32, name="result")
+            if c_tile % 2 == 0:
+                nc.vector.tensor_copy(out=result[:], in_=sums[:])
+            else:
+                nc.scalar.copy(out=result[:], in_=sums[:])
+            nc.sync.dma_start(out=out_rows[block(c_tile), half(h)], in_=result[:])
+
+        wq_grouped = turn_weight(nc, keep, psum, wq_rows, ident_f32, "wq")
+        wq_codes, wq_scales = quantise_weight(nc, keep, wq_grouped, "wq")
+        spread_biases()
+        first_sums = four_banks("q_sums")
+        regroup_x(0)
+        quantise_x(0, 0)
+        project_q(first_sums, 0, 0)
+        regroup_x(1)
+        quantise_x(0, 1)
+        quantise_x(1, 0)
+        project_q(first_sums, 0, 1)
+        quantise_x(1, 1)
+        first_best = tile_maximum(first_sums)
+        wv_grouped = turn_weight(nc, keep, psum, wv_rows, ident_f32, "wv")
+        partition_maximum(first_best, 0)
+        second_sums = four_banks("q_sums")
+        project_q(second_sums, 1, 0)
+        rows_of_q(0)
+        project_q(second_sums, 1, 1)
+        wv_codes, wv_scales = quantise_weight(nc, keep, wv_grouped, "wv")
+        second_best = tile_maximum(second_sums)
+
+        for g in range(PASSES):
+            for t in range(TILES):
+                attention_tile(g, t)
+                value_tile(g, t)
+                if g == 1 and t == TILES // 2 - 1:
+                    rows_of_q(1)
+            if g == 0:
+                partition_maximum(second_best, 1)
+            quantise_columns(nc, v_grouped, v_codes, v_scales, g, slice(0, OUT_CHANNELS))
+            quantise_columns(nc, att_grouped, att_codes, att_scales, g, half(0))
+
+        for g in range(PASSES):
+            for t in range(TILES):
+                attention_tile(g, TILES + t)
+                c_tile = g * 2 + t // 2
+                if t % 2 == 0:
+                    out_sums = psum.tile([P, HALF], F32, name="out_sums", tag="bank")
+                output_pass(out_sums, 0, c_tile, t % 2)
+                if t % 2 == 1:
+                    store_output(out_sums, 0, c_tile)
+            quantise_columns(nc, att_grouped, att_codes, att_scales, g, half(1))
+
+        last_sums = four_banks("out_sums")
+        for g in range(PASSES):
+            for c_tile in range(TILES):
+                output_pass(last_sums[c_tile], 1, c_tile, g)
+        for c_tile in range(TILES):
+            store_output(last_sums[c_tile], 1, c_tile)

@@ -113,13 +113,16 @@ def tile_cross_module_pa_kernel(tc, x1, wq1, bq1, wv1, bv1, k2, out):
 
         wq_rows = load_weight(nc, keep, wq1, "wq")
         x_sb = keep.tile([P, PASSES, PACK, PIXELS], BF16)
-        for g in range(PASSES):
-            for u in range(2):
-                first = g * K_PASS + u * 2 * P
-                nc.sync.dma_start(
-                    out=x_sb[:, g, 2 * u : 2 * u + 2, :],
-                    in_=x_rows[first : first + 2 * P, :].rearrange("(q e) n -> q e n", e=2),
-                )
+        for h in range(HALVES):
+            for g in range(PASSES):
+                for u in range(2):
+                    first = g * K_PASS + u * 2 * P
+                    nc.sync.dma_start(
+                        out=x_sb[:, g, 2 * u : 2 * u + 2, h * HALF : (h + 1) * HALF],
+                        in_=x_rows[first : first + 2 * P, h * HALF : (h + 1) * HALF].rearrange(
+                            "(q e) n -> q e n", e=2
+                        ),
+                    )
         wv_rows = load_weight(nc, keep, wv1, "wv")
 
         x_grouped = keep.tile([P, PASSES, PIXELS, PACK], BF16, align_bytes=64)
@@ -151,14 +154,13 @@ def tile_cross_module_pa_kernel(tc, x1, wq1, bq1, wv1, bv1, k2, out):
             nc.tensor.matmul(out=bv_bank[:], lhsT=ones[:], rhs=bv_row[:], start=True, stop=True)
             nc.scalar.copy(out=bv_all[:], in_=bv_bank[:])
 
-        def regroup_x(g):
-            for h in range(HALVES):
-                regrouped = x_grouped[:, g, half(h), :].rearrange("p (n i) t -> p n t i", i=4)
-                as_loaded = x_sb[:, g, :, half(h)].rearrange("p t (n i) -> p n t i", i=4)
-                if h == 0:
-                    nc.vector.tensor_copy(out=regrouped, in_=as_loaded)
-                else:
-                    nc.scalar.copy(out=regrouped, in_=as_loaded)
+        def regroup_x(g, h):
+            regrouped = x_grouped[:, g, half(h), :].rearrange("p (n i) t -> p n t i", i=4)
+            as_loaded = x_sb[:, g, :, half(h)].rearrange("p t (n i) -> p n t i", i=4)
+            if h == 0:
+                nc.vector.tensor_copy(out=regrouped, in_=as_loaded)
+            else:
+                nc.scalar.copy(out=regrouped, in_=as_loaded)
 
         def quantise_x(g, h):
             quantise_columns(nc, x_grouped, x_codes, x_scales, g, half(h))
@@ -266,52 +268,60 @@ def tile_cross_module_pa_kernel(tc, x1, wq1, bq1, wv1, bv1, k2, out):
             nc.sync.dma_start(out=out_rows[block(c_tile), half(h)], in_=result[:])
 
         wq_grouped = turn_weight(nc, keep, psum, wq_rows, ident_f32, "wq")
-        wq_codes, wq_scales = quantise_weight(nc, keep, wq_grouped, "wq")
         spread_biases()
         first_sums = four_banks("q_sums")
-        regroup_x(0)
+        regroup_x(0, 0)
+        wq_codes, wq_scales = quantise_weight(nc, keep, wq_grouped, "wq")
+        regroup_x(1, 0)
         quantise_x(0, 0)
         project_q(first_sums, 0, 0)
-        regroup_x(1)
-        quantise_x(0, 1)
         quantise_x(1, 0)
         project_q(first_sums, 0, 1)
-        quantise_x(1, 1)
+        regroup_x(0, 1)
+        quantise_x(0, 1)
         first_best = tile_maximum(first_sums)
+        regroup_x(1, 1)
+        quantise_x(1, 1)
         wv_grouped = turn_weight(nc, keep, psum, wv_rows, ident_f32, "wv")
         partition_maximum(first_best, 0)
         second_sums = four_banks("q_sums")
         project_q(second_sums, 1, 0)
-        rows_of_q(0)
         project_q(second_sums, 1, 1)
         wv_codes, wv_scales = quantise_weight(nc, keep, wv_grouped, "wv")
         second_best = tile_maximum(second_sums)
+        rows_of_q(0)
 
-        for g in range(PASSES):
-            for t in range(TILES):
+        def first_half_rounds(g, tiles):
+            for t in tiles:
                 attention_tile(g, t)
                 value_tile(g, t)
-                if g == 1 and t == TILES // 2 - 1:
-                    rows_of_q(1)
-            if g == 0:
-                partition_maximum(second_best, 1)
-            quantise_columns(nc, v_grouped, v_codes, v_scales, g, slice(0, OUT_CHANNELS))
-            quantise_columns(nc, att_grouped, att_codes, att_scales, g, half(0))
 
+        first_half_rounds(0, (0, 1))
+        partition_maximum(second_best, 1)
+        first_half_rounds(0, (2, 3))
+        quantise_columns(nc, v_grouped, v_codes, v_scales, 0, slice(0, OUT_CHANNELS))
+        quantise_columns(nc, att_grouped, att_codes, att_scales, 0, half(0))
+        first_half_rounds(1, (0, 1))
+        rows_of_q(1)
+        first_half_rounds(1, (2, 3))
+        quantise_columns(nc, v_grouped, v_codes, v_scales, 1, slice(0, OUT_CHANNELS))
+        quantise_columns(nc, att_grouped, att_codes, att_scales, 1, half(0))
+
+        first_out = four_banks("out_sums")
         for g in range(PASSES):
             for t in range(TILES):
                 attention_tile(g, TILES + t)
-                c_tile = g * 2 + t // 2
-                if t % 2 == 0:
-                    out_sums = psum.tile([P, HALF], F32, name="out_sums", tag="bank")
-                output_pass(out_sums, 0, c_tile, t % 2)
-                if t % 2 == 1:
-                    store_output(out_sums, 0, c_tile)
-            quantise_columns(nc, att_grouped, att_codes, att_scales, g, half(1))
+                output_pass(first_out[t], 0, t, g)
+                if g == PASSES - 1:
+                    store_output(first_out[t], 0, t)
+            if g == 0:
+                quantise_columns(nc, att_grouped, att_codes, att_scales, 0, half(1))
 
-        last_sums = four_banks("out_sums")
-        for g in range(PASSES):
-            for c_tile in range(TILES):
-                output_pass(last_sums[c_tile], 1, c_tile, g)
+        second_out = four_banks("out_sums")
         for c_tile in range(TILES):
-            store_output(last_sums[c_tile], 1, c_tile)
+            output_pass(second_out[c_tile], 1, c_tile, 0)
+        quantise_columns(nc, att_grouped, att_codes, att_scales, 1, half(1))
+        for c_tile in range(TILES):
+            output_pass(second_out[c_tile], 1, c_tile, 1)
+        for c_tile in range(TILES):
+            store_output(second_out[c_tile], 1, c_tile)

@@ -31,21 +31,18 @@ FLOPS = 3 * 2 * OUT_CHANNELS * CHANNELS * PIXELS
 
 def load_weight(nc, keep, weight, label):
     rows = keep.tile([P, TILES * CHANNELS], BF16, name=label + "_rows")
-    by_tile = rows[:].rearrange("p (t c) -> p t c", t=TILES)
-    for first in range(0, TILES, 2):
-        nc.sync.dma_start(
-            out=by_tile[:, first : first + 2, :],
-            in_=weight[first * P : (first + 2) * P, :].rearrange("(t p) c -> p t c", p=P),
-        )
+    nc.sync.dma_start(
+        out=rows[:].rearrange("p (t c) -> p t c", t=TILES),
+        in_=weight.rearrange("(t p) c -> p t c", p=P),
+    )
     return rows
 
 
-def turn_weight(nc, keep, psum, rows, ident_f32, label):
+def turn_weight(nc, psum, rows, grouped, ident_f32, tiles):
     words = rows[:].bitcast(F32)
-    grouped = keep.tile([P, PASSES * OUT_CHANNELS * PACK], BF16, name=label + "_grouped", align_bytes=64)
     grouped_words = grouped[:].bitcast(F32).rearrange("p (g o u) -> p g o u", g=PASSES, u=2)
-    for t in range(TILES):
-        turned = psum.tile([P, PASSES * 2, P], F32, name=label + "_turned", tag="bank")
+    for t in tiles:
+        turned = psum.tile([P, PASSES * 2, P], F32, name="turned", tag="bank")
         for b in range(PASSES * 2):
             first_word = (t * PASSES * 2 + b) * P
             nc.tensor.transpose(turned[:, b, :], words[:, first_word : first_word + P], ident_f32[:])
@@ -53,7 +50,6 @@ def turn_weight(nc, keep, psum, rows, ident_f32, label):
             out=grouped_words[:, :, t * P : (t + 1) * P, :],
             in_=turned[:].rearrange("p (g u) o -> p g o u", u=2),
         )
-    return grouped
 
 
 def quantise_weight(nc, keep, grouped, label):
@@ -95,14 +91,14 @@ def tile_cross_module_pa_kernel(tc, x1, wq1, bq1, wv1, bv1, k2, out):
 
         bq_rows = keep.tile([P, P], BF16)
         nc.vector.memset(bq_rows[:], 0.0)
-        nc.scalar.dma_start(out=bq_rows[0:TILES, :], in_=bq1.rearrange("(t p) -> t p", p=P))
+        nc.gpsimd.dma_start(out=bq_rows[0:TILES, :], in_=bq1.rearrange("(t p) -> t p", p=P))
         bv_row = keep.tile([P, OUT_CHANNELS], BF16)
         nc.vector.memset(bv_row[:], 0.0)
-        nc.scalar.dma_start(out=bv_row[0:1, :], in_=bv1.rearrange("(r c) -> r c", r=1))
+        nc.gpsimd.dma_start(out=bv_row[0:1, :], in_=bv1.rearrange("(r c) -> r c", r=1))
         k2_rows = keep.tile([P, PIXELS], BF16)
         nc.vector.memset(k2_rows[:], 0.0)
         for piece in range(PIECES):
-            nc.scalar.dma_start(out=k2_rows[piece : piece + 1, :], in_=k2)
+            nc.gpsimd.dma_start(out=k2_rows[piece : piece + 1, :], in_=k2)
         q_pieces = keep.tile([P, HALVES * TILES, P], BF16)
         nc.vector.memset(q_pieces[:], 0.0)
 
@@ -113,18 +109,17 @@ def tile_cross_module_pa_kernel(tc, x1, wq1, bq1, wv1, bv1, k2, out):
 
         wq_rows = load_weight(nc, keep, wq1, "wq")
         x_sb = keep.tile([P, PASSES, PACK, PIXELS], BF16)
-        for h in range(HALVES):
-            for g in range(PASSES):
-                for u in range(2):
-                    first = g * K_PASS + u * 2 * P
-                    nc.sync.dma_start(
-                        out=x_sb[:, g, 2 * u : 2 * u + 2, h * HALF : (h + 1) * HALF],
-                        in_=x_rows[first : first + 2 * P, h * HALF : (h + 1) * HALF].rearrange(
-                            "(q e) n -> q e n", e=2
-                        ),
-                    )
+        for g in range(PASSES):
+            for u in range(2):
+                first = g * K_PASS + u * 2 * P
+                nc.sync.dma_start(
+                    out=x_sb[:, g, 2 * u : 2 * u + 2, :],
+                    in_=x_rows[first : first + 2 * P, :].rearrange("(q e) n -> q e n", e=2),
+                )
         wv_rows = load_weight(nc, keep, wv1, "wv")
 
+        wq_grouped = keep.tile([P, PASSES * OUT_CHANNELS * PACK], BF16, align_bytes=64)
+        wv_grouped = keep.tile([P, PASSES * OUT_CHANNELS * PACK], BF16, align_bytes=64)
         x_grouped = keep.tile([P, PASSES, PIXELS, PACK], BF16, align_bytes=64)
         x_codes = keep.tile([P, PASSES, PIXELS], U32, align_bytes=64)
         x_scales = keep.tile([P, PASSES, PIXELS], U8, align_bytes=64)
@@ -267,55 +262,63 @@ def tile_cross_module_pa_kernel(tc, x1, wq1, bq1, wv1, bv1, k2, out):
                 nc.scalar.copy(out=result[:], in_=sums[:])
             nc.sync.dma_start(out=out_rows[block(c_tile), half(h)], in_=result[:])
 
-        wq_grouped = turn_weight(nc, keep, psum, wq_rows, ident_f32, "wq")
+        turn_weight(nc, psum, wq_rows, wq_grouped, ident_f32, range(TILES))
         spread_biases()
         first_sums = four_banks("q_sums")
         regroup_x(0, 0)
+        regroup_x(0, 1)
         wq_codes, wq_scales = quantise_weight(nc, keep, wq_grouped, "wq")
-        regroup_x(1, 0)
         quantise_x(0, 0)
         project_q(first_sums, 0, 0)
-        quantise_x(1, 0)
-        project_q(first_sums, 0, 1)
-        regroup_x(0, 1)
-        quantise_x(0, 1)
-        first_best = tile_maximum(first_sums)
+        regroup_x(1, 0)
         regroup_x(1, 1)
+        quantise_x(0, 1)
+        quantise_x(1, 0)
+        turn_weight(nc, psum, wv_rows, wv_grouped, ident_f32, (0, 1))
+        project_q(first_sums, 0, 1)
         quantise_x(1, 1)
-        wv_grouped = turn_weight(nc, keep, psum, wv_rows, ident_f32, "wv")
-        partition_maximum(first_best, 0)
+        first_best = tile_maximum(first_sums)
+        turn_weight(nc, psum, wv_rows, wv_grouped, ident_f32, (2, 3))
         second_sums = four_banks("q_sums")
         project_q(second_sums, 1, 0)
-        project_q(second_sums, 1, 1)
         wv_codes, wv_scales = quantise_weight(nc, keep, wv_grouped, "wv")
+        partition_maximum(first_best, 0)
+        project_q(second_sums, 1, 1)
         second_best = tile_maximum(second_sums)
+        for c_tile in range(TILES):
+            value_tile(0, c_tile)
+        quantise_columns(nc, v_grouped, v_codes, v_scales, 0, slice(0, OUT_CHANNELS))
         rows_of_q(0)
 
-        def first_half_rounds(g, tiles):
-            for t in tiles:
-                attention_tile(g, t)
-                value_tile(g, t)
-
-        first_half_rounds(0, (0, 1))
+        attention_tile(0, 0)
+        attention_tile(0, 1)
         partition_maximum(second_best, 1)
-        first_half_rounds(0, (2, 3))
-        quantise_columns(nc, v_grouped, v_codes, v_scales, 0, slice(0, OUT_CHANNELS))
+        attention_tile(0, 2)
+        attention_tile(0, 3)
         quantise_columns(nc, att_grouped, att_codes, att_scales, 0, half(0))
-        first_half_rounds(1, (0, 1))
-        rows_of_q(1)
-        first_half_rounds(1, (2, 3))
+        value_tile(1, 0)
+        value_tile(1, 1)
+        attention_tile(1, 0)
+        attention_tile(1, 1)
+        value_tile(1, 2)
+        value_tile(1, 3)
         quantise_columns(nc, v_grouped, v_codes, v_scales, 1, slice(0, OUT_CHANNELS))
+        rows_of_q(1)
+        attention_tile(1, 2)
+        attention_tile(1, 3)
         quantise_columns(nc, att_grouped, att_codes, att_scales, 1, half(0))
 
-        first_out = four_banks("out_sums")
         for g in range(PASSES):
             for t in range(TILES):
                 attention_tile(g, TILES + t)
-                output_pass(first_out[t], 0, t, g)
-                if g == PASSES - 1:
-                    store_output(first_out[t], 0, t)
             if g == 0:
                 quantise_columns(nc, att_grouped, att_codes, att_scales, 0, half(1))
+        first_out = four_banks("out_sums")
+        for g in range(PASSES):
+            for c_tile in range(TILES):
+                output_pass(first_out[c_tile], 0, c_tile, g)
+        for c_tile in range(TILES):
+            store_output(first_out[c_tile], 0, c_tile)
 
         second_out = four_banks("out_sums")
         for c_tile in range(TILES):

@@ -197,7 +197,7 @@ def tile_cross_module_pa_kernel(tc, x1, wq1, bq1, wv1, bv1, k2, out):
             nc.vector.tensor_reduce(out=q_cols[:, tiles], in_=best_turned[:], axis=mybir.AxisListType.X, op=MAX)
             nc.vector.tensor_copy(out=q_pieces[:, tiles, 0], in_=q_cols[:, tiles])
             nc.vector.tensor_tensor(out=q_rest[:, tiles], in0=q_cols[:, tiles], in1=q_pieces[:, tiles, 0], op=SUBTRACT)
-            nc.vector.tensor_copy(out=q_pieces[:, tiles, 1], in_=q_rest[:, tiles])
+            nc.vector.tensor_tensor(out=q_pieces[:, tiles, 1], in0=q_cols[:, tiles], in1=q_pieces[:, tiles, 0], op=SUBTRACT)
             nc.vector.tensor_tensor(out=q_pieces[:, tiles, 2], in0=q_rest[:, tiles], in1=q_pieces[:, tiles, 1], op=SUBTRACT)
 
         def rows_of_q(h):
@@ -285,28 +285,29 @@ def tile_cross_module_pa_kernel(tc, x1, wq1, bq1, wv1, bv1, k2, out):
         partition_maximum(first_best, 0)
         project_q(second_sums, 1, 1)
         second_best = tile_maximum(second_sums)
-        for c_tile in range(TILES):
-            value_tile(0, c_tile)
-        quantise_columns(nc, v_grouped, v_codes, v_scales, 0, slice(0, OUT_CHANNELS))
+        value_tile(0, 0)
+        value_tile(0, 1)
         rows_of_q(0)
-
         attention_tile(0, 0)
         attention_tile(0, 1)
         partition_maximum(second_best, 1)
         attention_tile(0, 2)
         attention_tile(0, 3)
         quantise_columns(nc, att_grouped, att_codes, att_scales, 0, half(0))
-        value_tile(1, 0)
-        value_tile(1, 1)
+        value_tile(0, 2)
+        value_tile(0, 3)
+        quantise_columns(nc, v_grouped, v_codes, v_scales, 0, slice(0, OUT_CHANNELS))
         attention_tile(1, 0)
         attention_tile(1, 1)
-        value_tile(1, 2)
-        value_tile(1, 3)
-        quantise_columns(nc, v_grouped, v_codes, v_scales, 1, slice(0, OUT_CHANNELS))
+        value_tile(1, 0)
+        value_tile(1, 1)
         rows_of_q(1)
         attention_tile(1, 2)
         attention_tile(1, 3)
         quantise_columns(nc, att_grouped, att_codes, att_scales, 1, half(0))
+        value_tile(1, 2)
+        value_tile(1, 3)
+        quantise_columns(nc, v_grouped, v_codes, v_scales, 1, slice(0, OUT_CHANNELS))
 
         for g in range(PASSES):
             for t in range(TILES):

@@ -29,48 +29,6 @@ PIECES = 3
 FLOPS = 3 * 2 * OUT_CHANNELS * CHANNELS * PIXELS
 
 
-def load_weight(nc, keep, weight, label):
-    rows = keep.tile([P, TILES * CHANNELS], BF16, name=label + "_rows")
-    nc.sync.dma_start(
-        out=rows[:].rearrange("p (t c) -> p t c", t=TILES),
-        in_=weight.rearrange("(t p) c -> p t c", p=P),
-    )
-    return rows
-
-
-def turn_weight(nc, psum, rows, grouped, ident_f32, tiles):
-    words = rows[:].bitcast(F32)
-    grouped_words = grouped[:].bitcast(F32).rearrange("p (g o u) -> p g o u", g=PASSES, u=2)
-    for t in tiles:
-        turned = psum.tile([P, PASSES * 2, P], F32, name="turned", tag="bank")
-        for b in range(PASSES * 2):
-            first_word = (t * PASSES * 2 + b) * P
-            nc.tensor.transpose(turned[:, b, :], words[:, first_word : first_word + P], ident_f32[:])
-        nc.scalar.copy(
-            out=grouped_words[:, :, t * P : (t + 1) * P, :],
-            in_=turned[:].rearrange("p (g u) o -> p g o u", u=2),
-        )
-
-
-def quantise_weight(nc, keep, grouped, label):
-    codes = keep.tile([P, PASSES, OUT_CHANNELS], U32, name=label + "_codes", align_bytes=64)
-    scales = keep.tile([P, PASSES, OUT_CHANNELS], U8, name=label + "_scales", align_bytes=64)
-    nc.vector.quantize_mx(
-        out=codes[:].rearrange("p g o -> p (g o)").bitcast(FP8X4),
-        scales=scales[:].rearrange("p g o -> p (g o)"),
-        in_=grouped[:],
-    )
-    return codes, scales
-
-
-def quantise_columns(nc, grouped, codes, scales, g, columns):
-    nc.vector.quantize_mx(
-        out=codes[:, g, columns].bitcast(FP8X4),
-        scales=scales[:, g, columns],
-        in_=grouped[:, g, columns, :].rearrange("p n t -> p (n t)"),
-    )
-
-
 def tile_cross_module_pa_kernel(tc, x1, wq1, bq1, wv1, bv1, k2, out):
     nc = tc.nc
     x_rows = x1.rearrange("b c h w -> (b c) (h w)")
@@ -78,48 +36,62 @@ def tile_cross_module_pa_kernel(tc, x1, wq1, bq1, wv1, bv1, k2, out):
 
     with ExitStack() as ctx:
         keep = ctx.enter_context(tc.tile_pool(name="keep", bufs=1))
-        ring = ctx.enter_context(tc.tile_pool(name="ring", bufs=4))
+        ring = ctx.enter_context(tc.tile_pool(name="ring", bufs=12))
         psum = ctx.enter_context(tc.psum_pool(name="psum", bufs=8))
         ctx.enter_context(tc.manual_schedule())
 
-        ident_f32 = keep.tile([P, P], F32)
-        make_identity(nc, ident_f32[:])
-        ident_bf16 = keep.tile([P, P], BF16)
-        make_identity(nc, ident_bf16[:])
-        ones = keep.tile([P, P], BF16)
-        nc.vector.memset(ones[:], 1.0)
+        wq_rows = keep.tile([P, TILES, CHANNELS], BF16)
+        wq_view = wq1.rearrange("(p t) c -> p t c", t=TILES)
+        for t in range(0, TILES, 2):
+            nc.sync.dma_start(out=wq_rows[:, t : t + 2, :], in_=wq_view[:, t : t + 2, :])
+        wv_rows = keep.tile([P, TILES, CHANNELS], BF16)
+        x_raw = []
+        for g in range(PASSES):
+            x_raw.append([])
+            for h in range(HALVES):
+                x_raw[g].append(keep.tile([P, PACK, HALF], BF16, name="x_raw_%d_%d" % (g, h)))
 
-        bq_rows = keep.tile([P, P], BF16)
-        nc.vector.memset(bq_rows[:], 0.0)
-        nc.gpsimd.dma_start(out=bq_rows[0:TILES, :], in_=bq1.rearrange("(t p) -> t p", p=P))
-        bv_row = keep.tile([P, OUT_CHANNELS], BF16)
-        nc.vector.memset(bv_row[:], 0.0)
-        nc.gpsimd.dma_start(out=bv_row[0:1, :], in_=bv1.rearrange("(r c) -> r c", r=1))
-        k2_rows = keep.tile([P, PIXELS], BF16)
-        nc.vector.memset(k2_rows[:], 0.0)
-        for piece in range(PIECES):
-            nc.gpsimd.dma_start(out=k2_rows[piece : piece + 1, :], in_=k2)
-        q_pieces = keep.tile([P, HALVES * TILES, P], BF16)
-        nc.vector.memset(q_pieces[:], 0.0)
+        def load_x(g, h):
+            nc.sync.dma_start(
+                out=x_raw[g][h][:],
+                in_=x_rows[g * K_PASS : (g + 1) * K_PASS, h * HALF : (h + 1) * HALF].rearrange("(p t) n -> p t n", t=PACK),
+            )
+
+        load_x(0, 0)
+        load_x(1, 0)
 
         warm_in = keep.tile([P, 1], F32)
         nc.vector.memset(warm_in[:], 0.0)
         warm_out = keep.tile([P, 1], F32)
         nc.scalar.activation(out=warm_out[:], in_=warm_in[:], func=SIGMOID)
+        ident_f32 = keep.tile([P, P], F32)
+        make_identity(nc, ident_f32[:])
+        ident_bf16 = keep.tile([P, P], BF16)
+        make_identity(nc, ident_bf16[:])
+        ones = keep.tile([P, P], BF16)
 
-        wq_rows = load_weight(nc, keep, wq1, "wq")
-        x_sb = keep.tile([P, PASSES, PACK, PIXELS], BF16)
-        for g in range(PASSES):
-            for u in range(2):
-                first = g * K_PASS + u * 2 * P
-                nc.sync.dma_start(
-                    out=x_sb[:, g, 2 * u : 2 * u + 2, :],
-                    in_=x_rows[first : first + 2 * P, :].rearrange("(q e) n -> q e n", e=2),
-                )
-        wv_rows = load_weight(nc, keep, wv1, "wv")
+        bq_cols = keep.tile([P, TILES], BF16)
+        nc.scalar.dma_start(out=bq_cols[:], in_=bq1.rearrange("(p t) -> p t", t=TILES))
+        bv_row = keep.tile([P, OUT_CHANNELS], BF16)
+        nc.vector.memset(bv_row[:].bitcast(F32), 0.0)
+        nc.scalar.dma_start(out=bv_row[0:1, :], in_=bv1.rearrange("(r c) -> r c", r=1))
+        k2_rows = keep.tile([P, PIXELS], BF16)
+        nc.vector.memset(k2_rows[:].bitcast(F32), 0.0)
+        nc.scalar.dma_start(out=k2_rows[0:PIECES, :], in_=k2.rearrange("b n -> (b n)").partition_broadcast(PIECES))
+        nc.vector.memset(ones[:], 1.0)
+        q_pieces = keep.tile([P, HALVES * TILES, P], BF16)
+        nc.gpsimd.memset(q_pieces[:].rearrange("p t n -> p (t n)").bitcast(F32), 0.0)
 
-        wq_grouped = keep.tile([P, PASSES * OUT_CHANNELS * PACK], BF16, align_bytes=64)
-        wv_grouped = keep.tile([P, PASSES * OUT_CHANNELS * PACK], BF16, align_bytes=64)
+        nc.sync.dma_start(out=wv_rows[:], in_=wv1.rearrange("(t p) c -> p t c", p=P))
+        load_x(0, 1)
+        load_x(1, 1)
+
+        wq_grouped = keep.tile([P, TILES, PASSES, P, PACK], BF16, align_bytes=64)
+        wq_codes = keep.tile([P, TILES, PASSES, P], U32, align_bytes=64)
+        wq_scales = keep.tile([P, TILES, PASSES, P], U8, align_bytes=64)
+        wv_grouped = keep.tile([P, TILES, PASSES, P, PACK], BF16, align_bytes=64)
+        wv_codes = keep.tile([P, TILES, PASSES, P], U32, align_bytes=64)
+        wv_scales = keep.tile([P, TILES, PASSES, P], U8, align_bytes=64)
         x_grouped = keep.tile([P, PASSES, PIXELS, PACK], BF16, align_bytes=64)
         x_codes = keep.tile([P, PASSES, PIXELS], U32, align_bytes=64)
         x_scales = keep.tile([P, PASSES, PIXELS], U8, align_bytes=64)
@@ -129,7 +101,6 @@ def tile_cross_module_pa_kernel(tc, x1, wq1, bq1, wv1, bv1, k2, out):
         v_grouped = keep.tile([P, PASSES, OUT_CHANNELS, PACK], BF16, align_bytes=64)
         v_codes = keep.tile([P, PASSES, OUT_CHANNELS], U32, align_bytes=64)
         v_scales = keep.tile([P, PASSES, OUT_CHANNELS], U8, align_bytes=64)
-        bq_cols = keep.tile([P, TILES], F32)
         bv_all = keep.tile([P, OUT_CHANNELS], F32)
         q_cols = keep.tile([P, HALVES * TILES], F32)
         q_rest = keep.tile([P, HALVES * TILES], F32)
@@ -141,63 +112,109 @@ def tile_cross_module_pa_kernel(tc, x1, wq1, bq1, wv1, bv1, k2, out):
         def block(t):
             return slice(t * P, (t + 1) * P)
 
-        def spread_biases():
-            bq_turned = psum.tile([P, P], BF16, tag="bank")
-            nc.tensor.transpose(bq_turned[:], bq_rows[:], ident_bf16[:])
-            nc.scalar.copy(out=bq_cols[:], in_=bq_turned[:, 0:TILES])
+        def turn(rows, grouped, t, on_scalar):
+            words = rows[:, t, :].bitcast(F32)
+            turned = psum.tile([P, PASSES * 2, P], F32, name="turned", tag="bank")
+            for g in range(PASSES):
+                for u in range(2):
+                    nc.tensor.transpose(
+                        turned[:, 2 * g + u, :], words[:, g * 256 + u : (g + 1) * 256 : 2], ident_f32[:]
+                    )
+            grouped_words = grouped[:, t].rearrange("p g o k -> p (g o k)").bitcast(F32).rearrange("p (g o u) -> p g o u", g=PASSES, u=2)
+            turned_words = turned[:].rearrange("p (g u) o -> p g o u", u=2)
+            if on_scalar:
+                nc.scalar.copy(out=grouped_words, in_=turned_words)
+            else:
+                nc.vector.tensor_copy(out=grouped_words, in_=turned_words)
+
+        def quantise_weight(grouped, codes, scales, t):
+            nc.vector.quantize_mx(
+                out=codes[:, t].rearrange("p g o -> p (g o)").bitcast(FP8X4),
+                scales=scales[:, t].rearrange("p g o -> p (g o)"),
+                in_=grouped[:, t].rearrange("p g o k -> p (g o k)"),
+            )
+
+        def spread_bv():
             bv_bank = psum.tile([P, OUT_CHANNELS], F32, tag="bank")
             nc.tensor.matmul(out=bv_bank[:], lhsT=ones[:], rhs=bv_row[:], start=True, stop=True)
             nc.scalar.copy(out=bv_all[:], in_=bv_bank[:])
 
-        def regroup_x(g, h):
-            regrouped = x_grouped[:, g, half(h), :].rearrange("p (n i) t -> p n t i", i=4)
-            as_loaded = x_sb[:, g, :, half(h)].rearrange("p t (n i) -> p n t i", i=4)
-            if h == 0:
-                nc.vector.tensor_copy(out=regrouped, in_=as_loaded)
-            else:
+        def regroup_x(g, h, first, last, on_scalar):
+            start = h * HALF
+            regrouped = x_grouped[:, g, start + first : start + last, :].rearrange("p (n i) t -> p n t i", i=4)
+            as_loaded = x_raw[g][h][:, :, first:last].rearrange("p t (n i) -> p n t i", i=4)
+            if on_scalar:
                 nc.scalar.copy(out=regrouped, in_=as_loaded)
+            else:
+                nc.vector.tensor_copy(out=regrouped, in_=as_loaded)
+
+        def quantise_columns(grouped, codes, scales, g, columns):
+            nc.vector.quantize_mx(
+                out=codes[:, g, columns].bitcast(FP8X4),
+                scales=scales[:, g, columns],
+                in_=grouped[:, g, columns, :].rearrange("p n t -> p (n t)"),
+            )
 
         def quantise_x(g, h):
-            quantise_columns(nc, x_grouped, x_codes, x_scales, g, half(h))
+            quantise_columns(x_grouped, x_codes, x_scales, g, half(h))
 
-        def project_q(sums, h, g):
+        def quantise_v(g):
+            quantise_columns(v_grouped, v_codes, v_scales, g, slice(0, OUT_CHANNELS))
+
+        def quantise_att(g, columns):
+            quantise_columns(att_grouped, att_codes, att_scales, g, columns)
+
+        def project_q(sums, h, g, t):
+            nc.tensor.matmul_mx(
+                out=sums[t][:],
+                lhsT=wq_codes[:, t, g, :].bitcast(FP8X4),
+                lhsT_scale=wq_scales[:, t, g, :],
+                rhs=x_codes[:, g, half(h)].bitcast(FP8X4),
+                rhs_scale=x_scales[:, g, half(h)],
+                start=(g == 0),
+                stop=(g == PASSES - 1),
+            )
+
+        def banks(label, width):
+            made = []
             for t in range(TILES):
-                nc.tensor.matmul_mx(
-                    out=sums[t][:],
-                    lhsT=wq_codes[:, g, block(t)].bitcast(FP8X4),
-                    lhsT_scale=wq_scales[:, g, block(t)],
-                    rhs=x_codes[:, g, half(h)].bitcast(FP8X4),
-                    rhs_scale=x_scales[:, g, half(h)],
-                    start=(g == 0),
-                    stop=(g == PASSES - 1),
-                )
+                made.append(psum.tile([P, width], F32, name=label, tag="bank"))
+            return made
 
-        def four_banks(label):
-            banks = []
-            for t in range(TILES):
-                banks.append(psum.tile([P, HALF], F32, name=label, tag="bank"))
-            return banks
-
-        def tile_maximum(sums):
+        def max_first(sums):
             best = ring.tile([P, HALF], F32, name="best")
             nc.scalar.activation(out=best[:], in_=sums[0][:], func=IDENTITY, bias=bq_cols[:, 0:1])
-            for t in range(1, TILES):
-                better = ring.tile([P, HALF], F32, name="best")
-                nc.vector.scalar_tensor_tensor(
-                    out=better[:], in0=sums[t][:], scalar=bq_cols[:, t : t + 1], in1=best[:], op0=ADD, op1=MAX
-                )
-                best = better
             return best
 
-        def partition_maximum(best, h):
-            tiles = slice(h * TILES, (h + 1) * TILES)
+        def max_next(sums, best, t):
+            better = ring.tile([P, HALF], F32, name="best")
+            nc.vector.scalar_tensor_tensor(
+                out=better[:], in0=sums[t][:], scalar=bq_cols[:, t : t + 1], in1=best[:], op0=ADD, op1=MAX
+            )
+            return better
+
+        def turn_best(best):
             best_turned = psum.tile([P, TILES, P], F32, tag="bank")
             for t in range(TILES):
                 nc.tensor.transpose(best_turned[:, t, :], best[:, block(t)], ident_f32[:])
-            nc.vector.tensor_reduce(out=q_cols[:, tiles], in_=best_turned[:], axis=mybir.AxisListType.X, op=MAX)
-            nc.vector.tensor_copy(out=q_pieces[:, tiles, 0], in_=q_cols[:, tiles])
+            return best_turned
+
+        def half_tiles(h):
+            return slice(h * TILES, (h + 1) * TILES)
+
+        def reduce_best(best_turned, h):
+            nc.vector.tensor_reduce(out=q_cols[:, half_tiles(h)], in_=best_turned[:], axis=mybir.AxisListType.X, op=MAX)
+
+        def piece_high(h):
+            nc.vector.tensor_copy(out=q_pieces[:, half_tiles(h), 0], in_=q_cols[:, half_tiles(h)])
+
+        def piece_middle(h):
+            tiles = half_tiles(h)
             nc.vector.tensor_tensor(out=q_rest[:, tiles], in0=q_cols[:, tiles], in1=q_pieces[:, tiles, 0], op=SUBTRACT)
             nc.vector.tensor_tensor(out=q_pieces[:, tiles, 1], in0=q_cols[:, tiles], in1=q_pieces[:, tiles, 0], op=SUBTRACT)
+
+        def piece_low(h):
+            tiles = half_tiles(h)
             nc.vector.tensor_tensor(out=q_pieces[:, tiles, 2], in0=q_rest[:, tiles], in1=q_pieces[:, tiles, 1], op=SUBTRACT)
 
         def rows_of_q(h):
@@ -223,7 +240,7 @@ def tile_cross_module_pa_kernel(tc, x1, wq1, bq1, wv1, bv1, k2, out):
                 scale=-1.0,
             )
 
-        def value_tile(g, c_tile):
+        def value_sums(g, c_tile):
             sums = psum.tile([P, PACK, P], F32, name="v_sums", tag="bank")
             for j in range(PACK):
                 for gc in range(PASSES):
@@ -231,11 +248,14 @@ def tile_cross_module_pa_kernel(tc, x1, wq1, bq1, wv1, bv1, k2, out):
                         out=sums[:, j, :],
                         lhsT=x_codes[:, gc, block(g * PACK + j)].bitcast(FP8X4),
                         lhsT_scale=x_scales[:, gc, block(g * PACK + j)],
-                        rhs=wv_codes[:, gc, block(c_tile)].bitcast(FP8X4),
-                        rhs_scale=wv_scales[:, gc, block(c_tile)],
+                        rhs=wv_codes[:, c_tile, gc, :].bitcast(FP8X4),
+                        rhs_scale=wv_scales[:, c_tile, gc, :],
                         start=(gc == 0),
                         stop=(gc == PASSES - 1),
                     )
+            return sums
+
+        def value_add(sums, g, c_tile):
             nc.vector.tensor_tensor(
                 out=v_grouped[:, g, block(c_tile), :],
                 in0=sums[:].rearrange("p j c -> p c j"),
@@ -243,89 +263,139 @@ def tile_cross_module_pa_kernel(tc, x1, wq1, bq1, wv1, bv1, k2, out):
                 op=ADD,
             )
 
-        def output_pass(sums, h, c_tile, g):
+        def output_pass(sums, columns, c_tile, g):
             nc.tensor.matmul_mx(
-                out=sums[:],
+                out=sums[c_tile][:],
                 lhsT=v_codes[:, g, block(c_tile)].bitcast(FP8X4),
                 lhsT_scale=v_scales[:, g, block(c_tile)],
-                rhs=att_codes[:, g, half(h)].bitcast(FP8X4),
-                rhs_scale=att_scales[:, g, half(h)],
+                rhs=att_codes[:, g, columns].bitcast(FP8X4),
+                rhs_scale=att_scales[:, g, columns],
                 start=(g == 0),
                 stop=(g == PASSES - 1),
             )
 
-        def store_output(sums, h, c_tile):
-            result = ring.tile([P, HALF], F32, name="result")
-            if c_tile % 2 == 0:
-                nc.vector.tensor_copy(out=result[:], in_=sums[:])
+        def store_output(sums, columns, c_tile, on_scalar):
+            result = ring.tile([P, columns.stop - columns.start], F32, name="result")
+            if on_scalar:
+                nc.scalar.copy(out=result[:], in_=sums[c_tile][:])
             else:
-                nc.scalar.copy(out=result[:], in_=sums[:])
-            nc.sync.dma_start(out=out_rows[block(c_tile), half(h)], in_=result[:])
+                nc.vector.tensor_copy(out=result[:], in_=sums[c_tile][:])
+            nc.sync.dma_start(out=out_rows[block(c_tile), columns], in_=result[:])
 
-        turn_weight(nc, psum, wq_rows, wq_grouped, ident_f32, range(TILES))
-        spread_biases()
-        first_sums = four_banks("q_sums")
-        regroup_x(0, 0)
-        regroup_x(0, 1)
-        wq_codes, wq_scales = quantise_weight(nc, keep, wq_grouped, "wq")
+        turn(wq_rows, wq_grouped, 0, True)
+        turn(wq_rows, wq_grouped, 1, False)
+        turn(wq_rows, wq_grouped, 2, True)
+        quantise_weight(wq_grouped, wq_codes, wq_scales, 0)
+        turn(wq_rows, wq_grouped, 3, False)
+        quantise_weight(wq_grouped, wq_codes, wq_scales, 1)
+        quantise_weight(wq_grouped, wq_codes, wq_scales, 2)
+        quantise_weight(wq_grouped, wq_codes, wq_scales, 3)
+        for g in range(PASSES):
+            regroup_x(g, 0, 0, 256, False)
+            regroup_x(g, 0, 256, 512, True)
         quantise_x(0, 0)
-        project_q(first_sums, 0, 0)
-        regroup_x(1, 0)
-        regroup_x(1, 1)
-        quantise_x(0, 1)
+        spread_bv()
+        turn(wv_rows, wv_grouped, 0, True)
+        turn(wv_rows, wv_grouped, 1, True)
         quantise_x(1, 0)
-        turn_weight(nc, psum, wv_rows, wv_grouped, ident_f32, (0, 1))
-        project_q(first_sums, 0, 1)
+        sums0 = banks("q_sums", HALF)
+        for t in range(TILES):
+            project_q(sums0, 0, 0, t)
+        turn(wv_rows, wv_grouped, 2, True)
+        for t in range(TILES):
+            project_q(sums0, 0, 1, t)
+        quantise_weight(wv_grouped, wv_codes, wv_scales, 0)
+        quantise_weight(wv_grouped, wv_codes, wv_scales, 1)
+        quantise_weight(wv_grouped, wv_codes, wv_scales, 2)
+        best = max_first(sums0)
+        regroup_x(0, 1, 0, 128, False)
+        best = max_next(sums0, best, 1)
+        regroup_x(0, 1, 128, 512, True)
+        v00 = value_sums(0, 0)
+        v01 = value_sums(0, 1)
+        v02 = value_sums(0, 2)
+        value_add(v00, 0, 0)
+        best = max_next(sums0, best, 2)
+        regroup_x(1, 1, 0, 128, False)
+        regroup_x(1, 1, 128, 512, True)
+        best = max_next(sums0, best, 3)
+        quantise_x(0, 1)
+        best_turned = turn_best(best)
+        value_add(v01, 0, 1)
+        turn(wv_rows, wv_grouped, 3, True)
+        reduce_best(best_turned, 0)
         quantise_x(1, 1)
-        first_best = tile_maximum(first_sums)
-        turn_weight(nc, psum, wv_rows, wv_grouped, ident_f32, (2, 3))
-        second_sums = four_banks("q_sums")
-        project_q(second_sums, 1, 0)
-        wv_codes, wv_scales = quantise_weight(nc, keep, wv_grouped, "wv")
-        partition_maximum(first_best, 0)
-        project_q(second_sums, 1, 1)
-        second_best = tile_maximum(second_sums)
-        value_tile(0, 0)
-        value_tile(0, 1)
+        piece_high(0)
+        value_add(v02, 0, 2)
+        piece_middle(0)
+        quantise_weight(wv_grouped, wv_codes, wv_scales, 3)
+        sums1 = banks("q_sums", HALF)
+        for t in range(TILES):
+            for g in range(PASSES):
+                project_q(sums1, 1, g, t)
+        piece_low(0)
+        best = max_first(sums1)
         rows_of_q(0)
+        best = max_next(sums1, best, 1)
         attention_tile(0, 0)
-        attention_tile(0, 1)
-        partition_maximum(second_best, 1)
-        attention_tile(0, 2)
-        attention_tile(0, 3)
-        quantise_columns(nc, att_grouped, att_codes, att_scales, 0, half(0))
-        value_tile(0, 2)
-        value_tile(0, 3)
-        quantise_columns(nc, v_grouped, v_codes, v_scales, 0, slice(0, OUT_CHANNELS))
         attention_tile(1, 0)
+        v12 = value_sums(1, 2)
+        best = max_next(sums1, best, 2)
+        attention_tile(0, 1)
+        v11 = value_sums(1, 1)
+        value_add(v12, 1, 2)
+        best = max_next(sums1, best, 3)
         attention_tile(1, 1)
-        value_tile(1, 0)
-        value_tile(1, 1)
-        rows_of_q(1)
+        value_add(v11, 1, 1)
+        best_turned = turn_best(best)
+        attention_tile(0, 2)
+        reduce_best(best_turned, 1)
+        v03 = value_sums(0, 3)
+        piece_high(1)
         attention_tile(1, 2)
+        value_add(v03, 0, 3)
+        piece_middle(1)
+        v10 = value_sums(1, 0)
+        attention_tile(0, 3)
+        quantise_v(0)
+        piece_low(1)
+        v13 = value_sums(1, 3)
+        value_add(v10, 1, 0)
+        rows_of_q(1)
         attention_tile(1, 3)
-        quantise_columns(nc, att_grouped, att_codes, att_scales, 1, half(0))
-        value_tile(1, 2)
-        value_tile(1, 3)
-        quantise_columns(nc, v_grouped, v_codes, v_scales, 1, slice(0, OUT_CHANNELS))
-
+        value_add(v13, 1, 3)
+        quantise_att(0, half(0))
+        quantise_v(1)
+        quantise_att(1, half(0))
+        for m_tile in (4, 5):
+            for g in range(PASSES):
+                attention_tile(g, m_tile)
+        out0 = banks("out_sums", HALF)
+        for c_tile in range(TILES):
+            for g in range(PASSES):
+                output_pass(out0, half(0), c_tile, g)
         for g in range(PASSES):
-            for t in range(TILES):
-                attention_tile(g, TILES + t)
-            if g == 0:
-                quantise_columns(nc, att_grouped, att_codes, att_scales, 0, half(1))
-        first_out = four_banks("out_sums")
-        for g in range(PASSES):
-            for c_tile in range(TILES):
-                output_pass(first_out[c_tile], 0, c_tile, g)
+            for m_tile in (6, 7):
+                attention_tile(g, m_tile)
+        chunk1 = slice(512, 768)
+        chunk2 = slice(768, 1024)
+        store_output(out0, half(0), 0, False)
+        quantise_att(0, chunk1)
+        quantise_att(1, chunk1)
+        store_output(out0, half(0), 1, False)
+        store_output(out0, half(0), 2, False)
+        out1 = banks("out_sums", 256)
         for c_tile in range(TILES):
-            store_output(first_out[c_tile], 0, c_tile)
-
-        second_out = four_banks("out_sums")
+            for g in range(PASSES):
+                output_pass(out1, chunk1, c_tile, g)
+        store_output(out0, half(0), 3, True)
+        quantise_att(0, chunk2)
         for c_tile in range(TILES):
-            output_pass(second_out[c_tile], 1, c_tile, 0)
-        quantise_columns(nc, att_grouped, att_codes, att_scales, 1, half(1))
+            store_output(out1, chunk1, c_tile, c_tile % 2 == 0)
+        out2 = banks("out_sums", 256)
         for c_tile in range(TILES):
-            output_pass(second_out[c_tile], 1, c_tile, 1)
+            output_pass(out2, chunk2, c_tile, 0)
+        quantise_att(1, chunk2)
         for c_tile in range(TILES):
-            store_output(second_out[c_tile], 1, c_tile)
+            output_pass(out2, chunk2, c_tile, 1)
+            store_output(out2, chunk2, c_tile, c_tile % 2 == 0)

@@ -44,6 +44,7 @@ def tile_cross_module_pa_kernel(tc, x1, wq1, bq1, wv1, bv1, k2, out):
         wq_view = wq1.rearrange("(p t) c -> p t c", t=TILES)
         for t in range(0, TILES, 2):
             nc.sync.dma_start(out=wq_rows[:, t : t + 2, :], in_=wq_view[:, t : t + 2, :])
+        wv_view = wv1.rearrange("(t p) c -> p t c", p=P)
         wv_rows = keep.tile([P, TILES, CHANNELS], BF16)
         x_raw = []
         for g in range(PASSES):
@@ -52,10 +53,12 @@ def tile_cross_module_pa_kernel(tc, x1, wq1, bq1, wv1, bv1, k2, out):
                 x_raw[g].append(keep.tile([P, PACK, HALF], BF16, name="x_raw_%d_%d" % (g, h)))
 
         def load_x(g, h):
-            nc.sync.dma_start(
-                out=x_raw[g][h][:],
-                in_=x_rows[g * K_PASS : (g + 1) * K_PASS, h * HALF : (h + 1) * HALF].rearrange("(p t) n -> p t n", t=PACK),
-            )
+            for u in range(2):
+                first = g * K_PASS + u * 2 * P
+                nc.sync.dma_start(
+                    out=x_raw[g][h][:, 2 * u : 2 * u + 2, :],
+                    in_=x_rows[first : first + 2 * P, h * HALF : (h + 1) * HALF].rearrange("(q e) n -> q e n", e=2),
+                )
 
         load_x(0, 0)
         load_x(1, 0)
@@ -77,12 +80,13 @@ def tile_cross_module_pa_kernel(tc, x1, wq1, bq1, wv1, bv1, k2, out):
         nc.scalar.dma_start(out=bv_row[0:1, :], in_=bv1.rearrange("(r c) -> r c", r=1))
         k2_rows = keep.tile([P, PIXELS], BF16)
         nc.vector.memset(k2_rows[:].bitcast(F32), 0.0)
-        nc.scalar.dma_start(out=k2_rows[0:PIECES, :], in_=k2.rearrange("b n -> (b n)").partition_broadcast(PIECES))
+        nc.scalar.dma_start(out=k2_rows[0:4, :], in_=k2.rearrange("b n -> (b n)").partition_broadcast(4))
         nc.vector.memset(ones[:], 1.0)
         q_pieces = keep.tile([P, HALVES * TILES, P], BF16)
         nc.gpsimd.memset(q_pieces[:].rearrange("p t n -> p (t n)").bitcast(F32), 0.0)
 
-        nc.sync.dma_start(out=wv_rows[:], in_=wv1.rearrange("(t p) c -> p t c", p=P))
+        for t in range(0, TILES, 2):
+            nc.sync.dma_start(out=wv_rows[:, t : t + 2, :], in_=wv_view[:, t : t + 2, :])
         load_x(0, 1)
         load_x(1, 1)
 
@@ -115,11 +119,8 @@ def tile_cross_module_pa_kernel(tc, x1, wq1, bq1, wv1, bv1, k2, out):
         def turn(rows, grouped, t, on_scalar):
             words = rows[:, t, :].bitcast(F32)
             turned = psum.tile([P, PASSES * 2, P], F32, name="turned", tag="bank")
-            for g in range(PASSES):
-                for u in range(2):
-                    nc.tensor.transpose(
-                        turned[:, 2 * g + u, :], words[:, g * 256 + u : (g + 1) * 256 : 2], ident_f32[:]
-                    )
+            for b in range(PASSES * 2):
+                nc.tensor.transpose(turned[:, b, :], words[:, block(b)], ident_f32[:])
             grouped_words = grouped[:, t].rearrange("p g o k -> p (g o k)").bitcast(F32).rearrange("p (g o u) -> p g o u", g=PASSES, u=2)
             turned_words = turned[:].rearrange("p (g u) o -> p g o u", u=2)
             if on_scalar:
@@ -287,115 +288,119 @@ def tile_cross_module_pa_kernel(tc, x1, wq1, bq1, wv1, bv1, k2, out):
         turn(wq_rows, wq_grouped, 2, True)
         quantise_weight(wq_grouped, wq_codes, wq_scales, 0)
         turn(wq_rows, wq_grouped, 3, False)
+        regroup_x(0, 0, 0, 192, False)
+        regroup_x(0, 0, 192, 512, True)
         quantise_weight(wq_grouped, wq_codes, wq_scales, 1)
         quantise_weight(wq_grouped, wq_codes, wq_scales, 2)
         quantise_weight(wq_grouped, wq_codes, wq_scales, 3)
-        for g in range(PASSES):
-            regroup_x(g, 0, 0, 256, False)
-            regroup_x(g, 0, 256, 512, True)
+        regroup_x(1, 0, 0, 192, False)
+        regroup_x(1, 0, 192, 512, True)
         quantise_x(0, 0)
-        spread_bv()
         turn(wv_rows, wv_grouped, 0, True)
         turn(wv_rows, wv_grouped, 1, True)
         quantise_x(1, 0)
-        sums0 = banks("q_sums", HALF)
-        for t in range(TILES):
-            project_q(sums0, 0, 0, t)
-        turn(wv_rows, wv_grouped, 2, True)
-        for t in range(TILES):
-            project_q(sums0, 0, 1, t)
         quantise_weight(wv_grouped, wv_codes, wv_scales, 0)
-        quantise_weight(wv_grouped, wv_codes, wv_scales, 1)
-        quantise_weight(wv_grouped, wv_codes, wv_scales, 2)
-        best = max_first(sums0)
+        spread_bv()
+        sums0 = banks("q_sums", HALF)
+        for g in range(PASSES):
+            for t in range(TILES):
+                project_q(sums0, 0, g, t)
         regroup_x(0, 1, 0, 128, False)
-        best = max_next(sums0, best, 1)
+        quantise_weight(wv_grouped, wv_codes, wv_scales, 1)
+        best = max_first(sums0)
+        regroup_x(1, 1, 0, 128, False)
         regroup_x(0, 1, 128, 512, True)
+        best = max_next(sums0, best, 1)
+        turn(wv_rows, wv_grouped, 2, True)
+        turn(wv_rows, wv_grouped, 3, True)
+        regroup_x(1, 1, 128, 512, True)
+        best = max_next(sums0, best, 2)
         v00 = value_sums(0, 0)
         v01 = value_sums(0, 1)
-        v02 = value_sums(0, 2)
-        value_add(v00, 0, 0)
-        best = max_next(sums0, best, 2)
-        regroup_x(1, 1, 0, 128, False)
-        regroup_x(1, 1, 128, 512, True)
         best = max_next(sums0, best, 3)
         quantise_x(0, 1)
         best_turned = turn_best(best)
-        value_add(v01, 0, 1)
-        turn(wv_rows, wv_grouped, 3, True)
-        reduce_best(best_turned, 0)
-        quantise_x(1, 1)
-        piece_high(0)
-        value_add(v02, 0, 2)
-        piece_middle(0)
-        quantise_weight(wv_grouped, wv_codes, wv_scales, 3)
         sums1 = banks("q_sums", HALF)
         for t in range(TILES):
-            for g in range(PASSES):
-                project_q(sums1, 1, g, t)
+            project_q(sums1, 1, 0, t)
+        reduce_best(best_turned, 0)
+        piece_high(0)
+        piece_middle(0)
         piece_low(0)
-        best = max_first(sums1)
+        quantise_x(1, 1)
         rows_of_q(0)
-        best = max_next(sums1, best, 1)
+        for t in range(TILES):
+            project_q(sums1, 1, 1, t)
+        best = max_first(sums1)
+        value_add(v00, 0, 0)
         attention_tile(0, 0)
         attention_tile(1, 0)
-        v12 = value_sums(1, 2)
+        quantise_weight(wv_grouped, wv_codes, wv_scales, 2)
+        value_add(v01, 0, 1)
+        best = max_next(sums1, best, 1)
+        quantise_weight(wv_grouped, wv_codes, wv_scales, 3)
+        v02 = value_sums(0, 2)
         best = max_next(sums1, best, 2)
         attention_tile(0, 1)
-        v11 = value_sums(1, 1)
-        value_add(v12, 1, 2)
-        best = max_next(sums1, best, 3)
         attention_tile(1, 1)
-        value_add(v11, 1, 1)
+        v03 = value_sums(0, 3)
+        best = max_next(sums1, best, 3)
+        value_add(v02, 0, 2)
         best_turned = turn_best(best)
         attention_tile(0, 2)
-        reduce_best(best_turned, 1)
-        v03 = value_sums(0, 3)
-        piece_high(1)
         attention_tile(1, 2)
-        value_add(v03, 0, 3)
-        piece_middle(1)
         v10 = value_sums(1, 0)
-        attention_tile(0, 3)
-        quantise_v(0)
+        reduce_best(best_turned, 1)
+        piece_high(1)
+        piece_middle(1)
         piece_low(1)
-        v13 = value_sums(1, 3)
-        value_add(v10, 1, 0)
+        value_add(v03, 0, 3)
+        attention_tile(0, 3)
         rows_of_q(1)
         attention_tile(1, 3)
-        value_add(v13, 1, 3)
+        v11 = value_sums(1, 1)
+        value_add(v10, 1, 0)
+        attention_tile(0, 4)
+        attention_tile(1, 4)
+        quantise_v(0)
+        value_add(v11, 1, 1)
+        v12 = value_sums(1, 2)
+        attention_tile(0, 5)
+        value_add(v12, 1, 2)
+        v13 = value_sums(1, 3)
+        attention_tile(1, 5)
         quantise_att(0, half(0))
-        quantise_v(1)
+        value_add(v13, 1, 3)
         quantise_att(1, half(0))
-        for m_tile in (4, 5):
-            for g in range(PASSES):
-                attention_tile(g, m_tile)
-        out0 = banks("out_sums", HALF)
-        for c_tile in range(TILES):
-            for g in range(PASSES):
-                output_pass(out0, half(0), c_tile, g)
-        for g in range(PASSES):
-            for m_tile in (6, 7):
-                attention_tile(g, m_tile)
+        quantise_v(1)
         chunk1 = slice(512, 768)
         chunk2 = slice(768, 1024)
-        store_output(out0, half(0), 0, False)
+        attention_tile(0, 6)
+        attention_tile(0, 7)
+        out0 = banks("out_sums", HALF)
+        for c_tile in range(TILES):
+            output_pass(out0, half(0), c_tile, 0)
+        attention_tile(1, 6)
+        attention_tile(1, 7)
+        for c_tile in range(TILES):
+            output_pass(out0, half(0), c_tile, 1)
         quantise_att(0, chunk1)
         quantise_att(1, chunk1)
-        store_output(out0, half(0), 1, False)
-        store_output(out0, half(0), 2, False)
         out1 = banks("out_sums", 256)
+        store_output(out0, half(0), 0, False)
         for c_tile in range(TILES):
             for g in range(PASSES):
                 output_pass(out1, chunk1, c_tile, g)
-        store_output(out0, half(0), 3, True)
         quantise_att(0, chunk2)
-        for c_tile in range(TILES):
-            store_output(out1, chunk1, c_tile, c_tile % 2 == 0)
+        store_output(out0, half(0), 1, True)
+        store_output(out0, half(0), 2, False)
+        store_output(out0, half(0), 3, True)
+        quantise_att(1, chunk2)
         out2 = banks("out_sums", 256)
         for c_tile in range(TILES):
+            store_output(out1, chunk1, c_tile, c_tile % 2 == 1)
+        for c_tile in range(TILES):
             output_pass(out2, chunk2, c_tile, 0)
-        quantise_att(1, chunk2)
         for c_tile in range(TILES):
             output_pass(out2, chunk2, c_tile, 1)
             store_output(out2, chunk2, c_tile, c_tile % 2 == 0)

@@ -40,12 +40,6 @@ def tile_cross_module_pa_kernel(tc, x1, wq1, bq1, wv1, bv1, k2, out):
         psum = ctx.enter_context(tc.psum_pool(name="psum", bufs=8))
         ctx.enter_context(tc.manual_schedule())
 
-        wq_rows = keep.tile([P, TILES, CHANNELS], BF16)
-        wq_view = wq1.rearrange("(p t) c -> p t c", t=TILES)
-        for t in range(0, TILES, 2):
-            nc.sync.dma_start(out=wq_rows[:, t : t + 2, :], in_=wq_view[:, t : t + 2, :])
-        wv_view = wv1.rearrange("(t p) c -> p t c", p=P)
-        wv_rows = keep.tile([P, TILES, CHANNELS], BF16)
         x_raw = []
         for g in range(PASSES):
             x_raw.append([])
@@ -62,33 +56,39 @@ def tile_cross_module_pa_kernel(tc, x1, wq1, bq1, wv1, bv1, k2, out):
 
         load_x(0, 0)
         load_x(1, 0)
-
         warm_in = keep.tile([P, 1], F32)
         nc.vector.memset(warm_in[:], 0.0)
         warm_out = keep.tile([P, 1], F32)
         nc.scalar.activation(out=warm_out[:], in_=warm_in[:], func=SIGMOID)
+        bq_cols = keep.tile([P, TILES], BF16)
+        nc.scalar.dma_start(out=bq_cols[:], in_=bq1.rearrange("(p t) -> p t", t=TILES))
+        k2_rows = keep.tile([P, PIXELS], BF16)
+        nc.vector.memset(k2_rows[:].bitcast(F32), 0.0)
+        nc.scalar.dma_start(out=k2_rows[0:4, :], in_=k2.rearrange("b n -> (b n)").partition_broadcast(4))
+        wq_rows = keep.tile([P, TILES, CHANNELS], BF16)
+        wq_view = wq1.rearrange("(p t) c -> p t c", t=TILES)
+        for t in range(TILES):
+            nc.sync.dma_start(out=wq_rows[:, t, :], in_=wq_view[:, t, :])
+        load_x(0, 1)
+        load_x(1, 1)
+        wv_rows = keep.tile([P, TILES, CHANNELS], BF16)
+        wv_view = wv1.rearrange("(t p) c -> p t c", p=P)
+        for t in range(0, TILES, 2):
+            nc.sync.dma_start(out=wv_rows[:, t : t + 2, :], in_=wv_view[:, t : t + 2, :])
+        bv_all = keep.tile([P, OUT_CHANNELS], BF16)
+        nc.sync.dma_start(out=bv_all[:], in_=bv1.partition_broadcast(P))
+
+        warm_ones = keep.tile([P, 2 * P], F32)
+        nc.vector.memset(warm_ones[:], 1.0)
+        warm_bank = psum.tile([P, 2 * P], F32, tag="bank")
+        for step in range(3):
+            nc.tensor.matmul(out=warm_bank[:], lhsT=warm_ones[:, 0:P], rhs=warm_ones[:], start=True, stop=True)
         ident_f32 = keep.tile([P, P], F32)
         make_identity(nc, ident_f32[:])
         ident_bf16 = keep.tile([P, P], BF16)
         make_identity(nc, ident_bf16[:])
-        ones = keep.tile([P, P], BF16)
-
-        bq_cols = keep.tile([P, TILES], BF16)
-        nc.scalar.dma_start(out=bq_cols[:], in_=bq1.rearrange("(p t) -> p t", t=TILES))
-        bv_row = keep.tile([P, OUT_CHANNELS], BF16)
-        nc.vector.memset(bv_row[:].bitcast(F32), 0.0)
-        nc.scalar.dma_start(out=bv_row[0:1, :], in_=bv1.rearrange("(r c) -> r c", r=1))
-        k2_rows = keep.tile([P, PIXELS], BF16)
-        nc.vector.memset(k2_rows[:].bitcast(F32), 0.0)
-        nc.scalar.dma_start(out=k2_rows[0:4, :], in_=k2.rearrange("b n -> (b n)").partition_broadcast(4))
-        nc.vector.memset(ones[:], 1.0)
         q_pieces = keep.tile([P, HALVES * TILES, P], BF16)
         nc.gpsimd.memset(q_pieces[:].rearrange("p t n -> p (t n)").bitcast(F32), 0.0)
-
-        for t in range(0, TILES, 2):
-            nc.sync.dma_start(out=wv_rows[:, t : t + 2, :], in_=wv_view[:, t : t + 2, :])
-        load_x(0, 1)
-        load_x(1, 1)
 
         wq_grouped = keep.tile([P, TILES, PASSES, P, PACK], BF16, align_bytes=64)
         wq_codes = keep.tile([P, TILES, PASSES, P], U32, align_bytes=64)
@@ -105,7 +105,6 @@ def tile_cross_module_pa_kernel(tc, x1, wq1, bq1, wv1, bv1, k2, out):
         v_grouped = keep.tile([P, PASSES, OUT_CHANNELS, PACK], BF16, align_bytes=64)
         v_codes = keep.tile([P, PASSES, OUT_CHANNELS], U32, align_bytes=64)
         v_scales = keep.tile([P, PASSES, OUT_CHANNELS], U8, align_bytes=64)
-        bv_all = keep.tile([P, OUT_CHANNELS], F32)
         q_cols = keep.tile([P, HALVES * TILES], F32)
         q_rest = keep.tile([P, HALVES * TILES], F32)
         q_rows = keep.tile([P, PIXELS], BF16)
@@ -135,10 +134,18 @@ def tile_cross_module_pa_kernel(tc, x1, wq1, bq1, wv1, bv1, k2, out):
                 in_=grouped[:, t].rearrange("p g o k -> p (g o k)"),
             )
 
-        def spread_bv():
-            bv_bank = psum.tile([P, OUT_CHANNELS], F32, tag="bank")
-            nc.tensor.matmul(out=bv_bank[:], lhsT=ones[:], rhs=bv_row[:], start=True, stop=True)
-            nc.scalar.copy(out=bv_all[:], in_=bv_bank[:])
+        def keep_clock(passes):
+            idle_bank = psum.tile([P, PASSES * P], F32, tag="bank")
+            for step in range(passes):
+                nc.tensor.matmul_mx(
+                    out=idle_bank[:],
+                    lhsT=x_codes[:, 0, 0:P].bitcast(FP8X4),
+                    lhsT_scale=x_scales[:, 0, 0:P],
+                    rhs=x_codes[:, 0, 0 : 2 * P].bitcast(FP8X4),
+                    rhs_scale=x_scales[:, 0, 0 : 2 * P],
+                    start=True,
+                    stop=True,
+                )
 
         def regroup_x(g, h, first, last, on_scalar):
             start = h * HALF
@@ -283,40 +290,30 @@ def tile_cross_module_pa_kernel(tc, x1, wq1, bq1, wv1, bv1, k2, out):
                 nc.vector.tensor_copy(out=result[:], in_=sums[c_tile][:])
             nc.sync.dma_start(out=out_rows[block(c_tile), columns], in_=result[:])
 
-        turn(wq_rows, wq_grouped, 0, True)
-        turn(wq_rows, wq_grouped, 1, False)
-        turn(wq_rows, wq_grouped, 2, True)
-        quantise_weight(wq_grouped, wq_codes, wq_scales, 0)
-        turn(wq_rows, wq_grouped, 3, False)
-        regroup_x(0, 0, 0, 192, False)
-        regroup_x(0, 0, 192, 512, True)
-        quantise_weight(wq_grouped, wq_codes, wq_scales, 1)
-        quantise_weight(wq_grouped, wq_codes, wq_scales, 2)
-        quantise_weight(wq_grouped, wq_codes, wq_scales, 3)
-        regroup_x(1, 0, 0, 192, False)
-        regroup_x(1, 0, 192, 512, True)
+        regroup_x(0, 0, 0, 320, False)
+        regroup_x(0, 0, 320, 512, True)
+        regroup_x(1, 0, 0, 320, False)
+        regroup_x(1, 0, 320, 512, True)
         quantise_x(0, 0)
-        turn(wv_rows, wv_grouped, 0, True)
-        turn(wv_rows, wv_grouped, 1, True)
         quantise_x(1, 0)
-        quantise_weight(wv_grouped, wv_codes, wv_scales, 0)
-        spread_bv()
+        for t in range(TILES):
+            turn(wq_rows, wq_grouped, t, True)
+            if t in (1, 2):
+                keep_clock(2)
         sums0 = banks("q_sums", HALF)
-        for g in range(PASSES):
-            for t in range(TILES):
+        for t in range(TILES):
+            quantise_weight(wq_grouped, wq_codes, wq_scales, t)
+            for g in range(PASSES):
                 project_q(sums0, 0, g, t)
-        regroup_x(0, 1, 0, 128, False)
-        quantise_weight(wv_grouped, wv_codes, wv_scales, 1)
         best = max_first(sums0)
-        regroup_x(1, 1, 0, 128, False)
-        regroup_x(0, 1, 128, 512, True)
+        regroup_x(0, 1, 192, 512, True)
+        regroup_x(1, 1, 192, 512, True)
+        for t in range(TILES):
+            turn(wv_rows, wv_grouped, t, True)
+        regroup_x(0, 1, 0, 192, False)
         best = max_next(sums0, best, 1)
-        turn(wv_rows, wv_grouped, 2, True)
-        turn(wv_rows, wv_grouped, 3, True)
-        regroup_x(1, 1, 128, 512, True)
+        regroup_x(1, 1, 0, 192, False)
         best = max_next(sums0, best, 2)
-        v00 = value_sums(0, 0)
-        v01 = value_sums(0, 1)
         best = max_next(sums0, best, 3)
         quantise_x(0, 1)
         best_turned = turn_best(best)
@@ -324,55 +321,60 @@ def tile_cross_module_pa_kernel(tc, x1, wq1, bq1, wv1, bv1, k2, out):
         for t in range(TILES):
             project_q(sums1, 1, 0, t)
         reduce_best(best_turned, 0)
+        quantise_weight(wv_grouped, wv_codes, wv_scales, 0)
         piece_high(0)
+        quantise_weight(wv_grouped, wv_codes, wv_scales, 1)
         piece_middle(0)
         piece_low(0)
-        quantise_x(1, 1)
+        v00 = value_sums(0, 0)
         rows_of_q(0)
-        for t in range(TILES):
+        quantise_x(1, 1)
+        v01 = value_sums(0, 1)
+        value_add(v00, 0, 0)
+        for t in range(TILES - 1):
             project_q(sums1, 1, 1, t)
         best = max_first(sums1)
-        value_add(v00, 0, 0)
         attention_tile(0, 0)
         attention_tile(1, 0)
+        project_q(sums1, 1, 1, 3)
         quantise_weight(wv_grouped, wv_codes, wv_scales, 2)
         value_add(v01, 0, 1)
         best = max_next(sums1, best, 1)
         quantise_weight(wv_grouped, wv_codes, wv_scales, 3)
+        attention_tile(0, 1)
         v02 = value_sums(0, 2)
         best = max_next(sums1, best, 2)
-        attention_tile(0, 1)
         attention_tile(1, 1)
-        v03 = value_sums(0, 3)
+        attention_tile(0, 2)
         best = max_next(sums1, best, 3)
+        attention_tile(1, 2)
         value_add(v02, 0, 2)
         best_turned = turn_best(best)
-        attention_tile(0, 2)
-        attention_tile(1, 2)
-        v10 = value_sums(1, 0)
+        v03 = value_sums(0, 3)
+        attention_tile(0, 3)
         reduce_best(best_turned, 1)
+        v10 = value_sums(1, 0)
         piece_high(1)
         piece_middle(1)
         piece_low(1)
         value_add(v03, 0, 3)
-        attention_tile(0, 3)
-        rows_of_q(1)
         attention_tile(1, 3)
+        rows_of_q(1)
         v11 = value_sums(1, 1)
         value_add(v10, 1, 0)
+        quantise_v(0)
+        v12 = value_sums(1, 2)
+        value_add(v11, 1, 1)
         attention_tile(0, 4)
         attention_tile(1, 4)
-        quantise_v(0)
-        value_add(v11, 1, 1)
-        v12 = value_sums(1, 2)
-        attention_tile(0, 5)
         value_add(v12, 1, 2)
         v13 = value_sums(1, 3)
-        attention_tile(1, 5)
-        quantise_att(0, half(0))
+        attention_tile(0, 5)
         value_add(v13, 1, 3)
-        quantise_att(1, half(0))
+        quantise_att(0, half(0))
+        attention_tile(1, 5)
         quantise_v(1)
+        quantise_att(1, half(0))
         chunk1 = slice(512, 768)
         chunk2 = slice(768, 1024)
         attention_tile(0, 6)

@@ -62,6 +62,9 @@ def tile_cross_module_pa_kernel(tc, x1, wq1, bq1, wv1, bv1, k2, out):
         nc.scalar.activation(out=warm_out[:], in_=warm_in[:], func=SIGMOID)
         bq_cols = keep.tile([P, TILES], BF16)
         nc.scalar.dma_start(out=bq_cols[:], in_=bq1.rearrange("(p t) -> p t", t=TILES))
+        bv_row = keep.tile([P, OUT_CHANNELS], BF16)
+        nc.vector.memset(bv_row[:].bitcast(F32), 0.0)
+        nc.scalar.dma_start(out=bv_row[0:1, :], in_=bv1.rearrange("(r c) -> r c", r=1))
         k2_rows = keep.tile([P, PIXELS], BF16)
         nc.vector.memset(k2_rows[:].bitcast(F32), 0.0)
         nc.scalar.dma_start(out=k2_rows[0:4, :], in_=k2.rearrange("b n -> (b n)").partition_broadcast(4))
@@ -75,8 +78,6 @@ def tile_cross_module_pa_kernel(tc, x1, wq1, bq1, wv1, bv1, k2, out):
         wv_view = wv1.rearrange("(t p) c -> p t c", p=P)
         for t in range(0, TILES, 2):
             nc.sync.dma_start(out=wv_rows[:, t : t + 2, :], in_=wv_view[:, t : t + 2, :])
-        bv_all = keep.tile([P, OUT_CHANNELS], BF16)
-        nc.sync.dma_start(out=bv_all[:], in_=bv1.partition_broadcast(P))
 
         warm_ones = keep.tile([P, 2 * P], F32)
         nc.vector.memset(warm_ones[:], 1.0)
@@ -87,6 +88,8 @@ def tile_cross_module_pa_kernel(tc, x1, wq1, bq1, wv1, bv1, k2, out):
         make_identity(nc, ident_f32[:])
         ident_bf16 = keep.tile([P, P], BF16)
         make_identity(nc, ident_bf16[:])
+        ones = keep.tile([P, P], BF16)
+        nc.vector.memset(ones[:], 1.0)
         q_pieces = keep.tile([P, HALVES * TILES, P], BF16)
         nc.gpsimd.memset(q_pieces[:].rearrange("p t n -> p (t n)").bitcast(F32), 0.0)
 
@@ -102,9 +105,10 @@ def tile_cross_module_pa_kernel(tc, x1, wq1, bq1, wv1, bv1, k2, out):
         att_grouped = keep.tile([P, PASSES, PIXELS, PACK], BF16, align_bytes=64)
         att_codes = keep.tile([P, PASSES, PIXELS], U32, align_bytes=64)
         att_scales = keep.tile([P, PASSES, PIXELS], U8, align_bytes=64)
-        v_grouped = keep.tile([P, PASSES, OUT_CHANNELS, PACK], BF16, align_bytes=64)
-        v_codes = keep.tile([P, PASSES, OUT_CHANNELS], U32, align_bytes=64)
-        v_scales = keep.tile([P, PASSES, OUT_CHANNELS], U8, align_bytes=64)
+        v_grouped = keep.tile([P, TILES, PASSES, P, PACK], BF16, align_bytes=64)
+        v_codes = keep.tile([P, TILES, PASSES, P], U32, align_bytes=64)
+        v_scales = keep.tile([P, TILES, PASSES, P], U8, align_bytes=64)
+        bv_all = keep.tile([P, OUT_CHANNELS], F32)
         q_cols = keep.tile([P, HALVES * TILES], F32)
         q_rest = keep.tile([P, HALVES * TILES], F32)
         q_rows = keep.tile([P, PIXELS], BF16)
@@ -147,6 +151,14 @@ def tile_cross_module_pa_kernel(tc, x1, wq1, bq1, wv1, bv1, k2, out):
                     stop=True,
                 )
 
+        def bv_sums():
+            bv_bank = psum.tile([P, OUT_CHANNELS], F32, tag="bank")
+            nc.tensor.matmul(out=bv_bank[:], lhsT=ones[:], rhs=bv_row[:], start=True, stop=True)
+            return bv_bank
+
+        def bv_copy(bv_bank):
+            nc.scalar.copy(out=bv_all[:], in_=bv_bank[:])
+
         def regroup_x(g, h, first, last, on_scalar):
             start = h * HALF
             regrouped = x_grouped[:, g, start + first : start + last, :].rearrange("p (n i) t -> p n t i", i=4)
@@ -166,8 +178,8 @@ def tile_cross_module_pa_kernel(tc, x1, wq1, bq1, wv1, bv1, k2, out):
         def quantise_x(g, h):
             quantise_columns(x_grouped, x_codes, x_scales, g, half(h))
 
-        def quantise_v(g):
-            quantise_columns(v_grouped, v_codes, v_scales, g, slice(0, OUT_CHANNELS))
+        def quantise_v(c_tile):
+            quantise_weight(v_grouped, v_codes, v_scales, c_tile)
 
         def quantise_att(g, columns):
             quantise_columns(att_grouped, att_codes, att_scales, g, columns)
@@ -265,7 +277,7 @@ def tile_cross_module_pa_kernel(tc, x1, wq1, bq1, wv1, bv1, k2, out):
 
         def value_add(sums, g, c_tile):
             nc.vector.tensor_tensor(
-                out=v_grouped[:, g, block(c_tile), :],
+                out=v_grouped[:, c_tile, g],
                 in0=sums[:].rearrange("p j c -> p c j"),
                 in1=bv_all[:, block(c_tile)].unsqueeze(2).to_broadcast([P, P, PACK]),
                 op=ADD,
@@ -273,21 +285,24 @@ def tile_cross_module_pa_kernel(tc, x1, wq1, bq1, wv1, bv1, k2, out):
 
         def output_pass(sums, columns, c_tile, g):
             nc.tensor.matmul_mx(
-                out=sums[c_tile][:],
-                lhsT=v_codes[:, g, block(c_tile)].bitcast(FP8X4),
-                lhsT_scale=v_scales[:, g, block(c_tile)],
+                out=sums[:],
+                lhsT=v_codes[:, c_tile, g, :].bitcast(FP8X4),
+                lhsT_scale=v_scales[:, c_tile, g, :],
                 rhs=att_codes[:, g, columns].bitcast(FP8X4),
                 rhs_scale=att_scales[:, g, columns],
                 start=(g == 0),
                 stop=(g == PASSES - 1),
             )
 
+        def output_bank(columns):
+            return psum.tile([P, columns.stop - columns.start], F32, name="out_sums", tag="bank")
+
         def store_output(sums, columns, c_tile, on_scalar):
             result = ring.tile([P, columns.stop - columns.start], F32, name="result")
             if on_scalar:
-                nc.scalar.copy(out=result[:], in_=sums[c_tile][:])
+                nc.scalar.copy(out=result[:], in_=sums[:])
             else:
-                nc.vector.tensor_copy(out=result[:], in_=sums[c_tile][:])
+                nc.vector.tensor_copy(out=result[:], in_=sums[:])
             nc.sync.dma_start(out=out_rows[block(c_tile), columns], in_=result[:])
 
         regroup_x(0, 0, 0, 320, False)
@@ -308,8 +323,9 @@ def tile_cross_module_pa_kernel(tc, x1, wq1, bq1, wv1, bv1, k2, out):
         best = max_first(sums0)
         regroup_x(0, 1, 192, 512, True)
         regroup_x(1, 1, 192, 512, True)
-        for t in range(TILES):
-            turn(wv_rows, wv_grouped, t, True)
+        bv_bank = bv_sums()
+        turn(wv_rows, wv_grouped, 0, True)
+        turn(wv_rows, wv_grouped, 1, True)
         regroup_x(0, 1, 0, 192, False)
         best = max_next(sums0, best, 1)
         regroup_x(1, 1, 0, 192, False)
@@ -317,92 +333,105 @@ def tile_cross_module_pa_kernel(tc, x1, wq1, bq1, wv1, bv1, k2, out):
         best = max_next(sums0, best, 3)
         quantise_x(0, 1)
         best_turned = turn_best(best)
+        bv_copy(bv_bank)
         sums1 = banks("q_sums", HALF)
         for t in range(TILES):
             project_q(sums1, 1, 0, t)
+        quantise_x(1, 1)
+        for t in range(TILES):
+            project_q(sums1, 1, 1, t)
         reduce_best(best_turned, 0)
         quantise_weight(wv_grouped, wv_codes, wv_scales, 0)
         piece_high(0)
+        best = max_first(sums1)
         quantise_weight(wv_grouped, wv_codes, wv_scales, 1)
         piece_middle(0)
         piece_low(0)
-        v00 = value_sums(0, 0)
         rows_of_q(0)
-        quantise_x(1, 1)
-        v01 = value_sums(0, 1)
-        value_add(v00, 0, 0)
-        for t in range(TILES - 1):
-            project_q(sums1, 1, 1, t)
-        best = max_first(sums1)
+        v00 = value_sums(0, 0)
+        turn(wv_rows, wv_grouped, 2, True)
+        best = max_next(sums1, best, 1)
         attention_tile(0, 0)
         attention_tile(1, 0)
-        project_q(sums1, 1, 1, 3)
-        quantise_weight(wv_grouped, wv_codes, wv_scales, 2)
-        value_add(v01, 0, 1)
-        best = max_next(sums1, best, 1)
-        quantise_weight(wv_grouped, wv_codes, wv_scales, 3)
-        attention_tile(0, 1)
-        v02 = value_sums(0, 2)
         best = max_next(sums1, best, 2)
-        attention_tile(1, 1)
-        attention_tile(0, 2)
+        chunk1 = slice(512, 768)
+        chunk2 = slice(768, 1024)
+        attention_tile(0, 1)
         best = max_next(sums1, best, 3)
-        attention_tile(1, 2)
-        value_add(v02, 0, 2)
+        attention_tile(1, 1)
+        value_add(v00, 0, 0)
         best_turned = turn_best(best)
-        v03 = value_sums(0, 3)
-        attention_tile(0, 3)
-        reduce_best(best_turned, 1)
+        turn(wv_rows, wv_grouped, 3, True)
         v10 = value_sums(1, 0)
+        attention_tile(0, 2)
+        attention_tile(1, 2)
+        quantise_weight(wv_grouped, wv_codes, wv_scales, 2)
+        v01 = value_sums(0, 1)
+        reduce_best(best_turned, 1)
         piece_high(1)
         piece_middle(1)
         piece_low(1)
-        value_add(v03, 0, 3)
-        attention_tile(1, 3)
-        rows_of_q(1)
-        v11 = value_sums(1, 1)
+        attention_tile(0, 3)
         value_add(v10, 1, 0)
+        rows_of_q(1)
+        quantise_weight(wv_grouped, wv_codes, wv_scales, 3)
+        v11 = value_sums(1, 1)
+        value_add(v01, 0, 1)
         quantise_v(0)
-        v12 = value_sums(1, 2)
+        attention_tile(1, 3)
+        v02 = value_sums(0, 2)
         value_add(v11, 1, 1)
         attention_tile(0, 4)
         attention_tile(1, 4)
-        value_add(v12, 1, 2)
-        v13 = value_sums(1, 3)
-        attention_tile(0, 5)
-        value_add(v13, 1, 3)
-        quantise_att(0, half(0))
-        attention_tile(1, 5)
+        value_add(v02, 0, 2)
         quantise_v(1)
+        v12 = value_sums(1, 2)
+        attention_tile(0, 5)
+        quantise_att(0, half(0))
         quantise_att(1, half(0))
-        chunk1 = slice(512, 768)
-        chunk2 = slice(768, 1024)
+        attention_tile(1, 5)
+        value_add(v12, 1, 2)
+        v03 = value_sums(0, 3)
         attention_tile(0, 6)
+        out00 = output_bank(half(0))
+        output_pass(out00, half(0), 0, 0)
+        output_pass(out00, half(0), 0, 1)
+        value_add(v03, 0, 3)
+        quantise_v(2)
         attention_tile(0, 7)
-        out0 = banks("out_sums", HALF)
-        for c_tile in range(TILES):
-            output_pass(out0, half(0), c_tile, 0)
+        v13 = value_sums(1, 3)
+        store_output(out00, half(0), 0, False)
         attention_tile(1, 6)
+        out01 = output_bank(half(0))
+        output_pass(out01, half(0), 1, 0)
+        output_pass(out01, half(0), 1, 1)
+        value_add(v13, 1, 3)
         attention_tile(1, 7)
-        for c_tile in range(TILES):
-            output_pass(out0, half(0), c_tile, 1)
         quantise_att(0, chunk1)
+        quantise_v(3)
+        store_output(out01, half(0), 1, False)
+        out02 = output_bank(half(0))
+        output_pass(out02, half(0), 2, 0)
+        output_pass(out02, half(0), 2, 1)
         quantise_att(1, chunk1)
-        out1 = banks("out_sums", 256)
-        store_output(out0, half(0), 0, False)
-        for c_tile in range(TILES):
-            for g in range(PASSES):
-                output_pass(out1, chunk1, c_tile, g)
+        out03 = output_bank(half(0))
+        output_pass(out03, half(0), 3, 0)
+        output_pass(out03, half(0), 3, 1)
+        store_output(out02, half(0), 2, True)
         quantise_att(0, chunk2)
-        store_output(out0, half(0), 1, True)
-        store_output(out0, half(0), 2, False)
-        store_output(out0, half(0), 3, True)
+        out1 = []
+        for c_tile in range(TILES):
+            out1.append(output_bank(chunk1))
+            for g in range(PASSES):
+                output_pass(out1[c_tile], chunk1, c_tile, g)
         quantise_att(1, chunk2)
-        out2 = banks("out_sums", 256)
+        store_output(out03, half(0), 3, True)
+        out2 = []
         for c_tile in range(TILES):
-            store_output(out1, chunk1, c_tile, c_tile % 2 == 1)
+            store_output(out1[c_tile], chunk1, c_tile, c_tile % 2 == 1)
         for c_tile in range(TILES):
-            output_pass(out2, chunk2, c_tile, 0)
+            out2.append(output_bank(chunk2))
+            output_pass(out2[c_tile], chunk2, c_tile, 0)
         for c_tile in range(TILES):
-            output_pass(out2, chunk2, c_tile, 1)
-            store_output(out2, chunk2, c_tile, c_tile % 2 == 0)
+            output_pass(out2[c_tile], chunk2, c_tile, 1)
+            store_output(out2[c_tile], chunk2, c_tile, c_tile % 2 == 0)

@@ -79,11 +79,11 @@ def tile_cross_module_pa_kernel(tc, x1, wq1, bq1, wv1, bv1, k2, out):
         for t in range(0, TILES, 2):
             nc.sync.dma_start(out=wv_rows[:, t : t + 2, :], in_=wv_view[:, t : t + 2, :])
 
-        warm_ones = keep.tile([P, 2 * P], F32)
-        nc.vector.memset(warm_ones[:], 1.0)
-        warm_bank = psum.tile([P, 2 * P], F32, tag="bank")
-        for step in range(3):
-            nc.tensor.matmul(out=warm_bank[:], lhsT=warm_ones[:, 0:P], rhs=warm_ones[:], start=True, stop=True)
+        idle_values = keep.tile([P, 2 * P * PACK], BF16, align_bytes=64)
+        nc.vector.memset(idle_values[:].bitcast(F32), 0.0)
+        idle_codes = keep.tile([P, 2 * P], U32, align_bytes=64)
+        idle_scales = keep.tile([P, 2 * P], U8, align_bytes=64)
+        nc.vector.quantize_mx(out=idle_codes[:].bitcast(FP8X4), scales=idle_scales[:], in_=idle_values[:])
         ident_f32 = keep.tile([P, P], F32)
         make_identity(nc, ident_f32[:])
         ident_bf16 = keep.tile([P, P], BF16)
@@ -143,10 +143,10 @@ def tile_cross_module_pa_kernel(tc, x1, wq1, bq1, wv1, bv1, k2, out):
             for step in range(passes):
                 nc.tensor.matmul_mx(
                     out=idle_bank[:],
-                    lhsT=x_codes[:, 0, 0:P].bitcast(FP8X4),
-                    lhsT_scale=x_scales[:, 0, 0:P],
-                    rhs=x_codes[:, 0, 0 : 2 * P].bitcast(FP8X4),
-                    rhs_scale=x_scales[:, 0, 0 : 2 * P],
+                    lhsT=idle_codes[:, 0:P].bitcast(FP8X4),
+                    lhsT_scale=idle_scales[:, 0:P],
+                    rhs=idle_codes[:].bitcast(FP8X4),
+                    rhs_scale=idle_scales[:],
                     start=True,
                     stop=True,
                 )
@@ -305,6 +305,7 @@ def tile_cross_module_pa_kernel(tc, x1, wq1, bq1, wv1, bv1, k2, out):
                 nc.vector.tensor_copy(out=result[:], in_=sums[:])
             nc.sync.dma_start(out=out_rows[block(c_tile), columns], in_=result[:])
 
+        keep_clock(12)
         regroup_x(0, 0, 0, 320, False)
         regroup_x(0, 0, 320, 512, True)
         regroup_x(1, 0, 0, 320, False)
@@ -313,8 +314,8 @@ def tile_cross_module_pa_kernel(tc, x1, wq1, bq1, wv1, bv1, k2, out):
         quantise_x(1, 0)
         for t in range(TILES):
             turn(wq_rows, wq_grouped, t, True)
-            if t in (1, 2):
-                keep_clock(2)
+            if t < 3:
+                keep_clock(1)
         sums0 = banks("q_sums", HALF)
         for t in range(TILES):
             quantise_weight(wq_grouped, wq_codes, wq_scales, t)
@@ -324,8 +325,10 @@ def tile_cross_module_pa_kernel(tc, x1, wq1, bq1, wv1, bv1, k2, out):
         regroup_x(0, 1, 192, 512, True)
         regroup_x(1, 1, 192, 512, True)
         bv_bank = bv_sums()
+        keep_clock(4)
         turn(wv_rows, wv_grouped, 0, True)
         turn(wv_rows, wv_grouped, 1, True)
+        keep_clock(2)
         regroup_x(0, 1, 0, 192, False)
         best = max_next(sums0, best, 1)
         regroup_x(1, 1, 0, 192, False)

@@ -24,6 +24,7 @@ PASSES = 2
 HALF = 512
 HALVES = PIXELS // HALF
 TILES = OUT_CHANNELS // P
+CHUNKS = ((0, 4), (4, 6), (6, 8))
 PIECES = 3
 
 FLOPS = 3 * 2 * OUT_CHANNELS * CHANNELS * PIXELS
@@ -102,15 +103,22 @@ def tile_cross_module_pa_kernel(tc, x1, wq1, bq1, wv1, bv1, k2, out):
         x_grouped = keep.tile([P, PASSES, PIXELS, PACK], BF16, align_bytes=64)
         x_codes = keep.tile([P, PASSES, PIXELS], U32, align_bytes=64)
         x_scales = keep.tile([P, PASSES, PIXELS], U8, align_bytes=64)
-        att_grouped = keep.tile([P, PASSES, PIXELS, PACK], BF16, align_bytes=64)
-        att_codes = keep.tile([P, PASSES, PIXELS], U32, align_bytes=64)
-        att_scales = keep.tile([P, PASSES, PIXELS], U8, align_bytes=64)
+        att_grouped = []
+        att_codes = []
+        att_scales = []
+        for i in range(len(CHUNKS)):
+            width = (CHUNKS[i][1] - CHUNKS[i][0]) * P
+            att_grouped.append(keep.tile([P, PASSES, width, PACK], BF16, name="att_grouped_%d" % i, align_bytes=64))
+            att_codes.append(keep.tile([P, PASSES, width], U32, name="att_codes_%d" % i, align_bytes=64))
+            att_scales.append(keep.tile([P, PASSES, width], U8, name="att_scales_%d" % i, align_bytes=64))
         v_grouped = keep.tile([P, TILES, PASSES, P, PACK], BF16, align_bytes=64)
         v_codes = keep.tile([P, TILES, PASSES, P], U32, align_bytes=64)
         v_scales = keep.tile([P, TILES, PASSES, P], U8, align_bytes=64)
         bv_all = keep.tile([P, OUT_CHANNELS], F32)
         q_cols = keep.tile([P, HALVES * TILES], F32)
-        q_rest = keep.tile([P, HALVES * TILES], F32)
+        q_rest = []
+        for h in range(HALVES):
+            q_rest.append(keep.tile([P, TILES], F32, name="q_rest_%d" % h))
         q_rows = keep.tile([P, PIXELS], BF16)
 
         def half(h):
@@ -181,8 +189,17 @@ def tile_cross_module_pa_kernel(tc, x1, wq1, bq1, wv1, bv1, k2, out):
         def quantise_v(c_tile):
             quantise_weight(v_grouped, v_codes, v_scales, c_tile)
 
-        def quantise_att(g, columns):
-            quantise_columns(att_grouped, att_codes, att_scales, g, columns)
+        def quantise_att(i):
+            nc.vector.quantize_mx(
+                out=att_codes[i][:].rearrange("p g m -> p (g m)").bitcast(FP8X4),
+                scales=att_scales[i][:].rearrange("p g m -> p (g m)"),
+                in_=att_grouped[i][:].rearrange("p g m k -> p (g m k)"),
+            )
+
+        def chunk_of(m_tile):
+            for i in range(len(CHUNKS)):
+                if m_tile < CHUNKS[i][1]:
+                    return i
 
         def project_q(sums, h, g, t):
             nc.tensor.matmul_mx(
@@ -225,17 +242,25 @@ def tile_cross_module_pa_kernel(tc, x1, wq1, bq1, wv1, bv1, k2, out):
         def reduce_best(best_turned, h):
             nc.vector.tensor_reduce(out=q_cols[:, half_tiles(h)], in_=best_turned[:], axis=mybir.AxisListType.X, op=MAX)
 
+        def split_q(h, engine):
+            tiles = slice(h * TILES, (h + 1) * TILES)
+            engine.tensor_copy(out=q_pieces[:, tiles, 0], in_=q_cols[:, tiles])
+            engine.tensor_tensor(out=q_rest[h][:], in0=q_cols[:, tiles], in1=q_pieces[:, tiles, 0], op=SUBTRACT)
+            engine.tensor_tensor(out=q_pieces[:, tiles, 1], in0=q_cols[:, tiles], in1=q_pieces[:, tiles, 0], op=SUBTRACT)
+            engine.tensor_tensor(out=q_pieces[:, tiles, 2], in0=q_rest[h][:], in1=q_pieces[:, tiles, 1], op=SUBTRACT)
+
         def piece_high(h):
-            nc.vector.tensor_copy(out=q_pieces[:, half_tiles(h), 0], in_=q_cols[:, half_tiles(h)])
+            tiles = half_tiles(h)
+            nc.vector.tensor_copy(out=q_pieces[:, tiles, 0], in_=q_cols[:, tiles])
 
         def piece_middle(h):
             tiles = half_tiles(h)
-            nc.vector.tensor_tensor(out=q_rest[:, tiles], in0=q_cols[:, tiles], in1=q_pieces[:, tiles, 0], op=SUBTRACT)
+            nc.vector.tensor_tensor(out=q_rest[h][:], in0=q_cols[:, tiles], in1=q_pieces[:, tiles, 0], op=SUBTRACT)
             nc.vector.tensor_tensor(out=q_pieces[:, tiles, 1], in0=q_cols[:, tiles], in1=q_pieces[:, tiles, 0], op=SUBTRACT)
 
         def piece_low(h):
             tiles = half_tiles(h)
-            nc.vector.tensor_tensor(out=q_pieces[:, tiles, 2], in0=q_rest[:, tiles], in1=q_pieces[:, tiles, 1], op=SUBTRACT)
+            nc.vector.tensor_tensor(out=q_pieces[:, tiles, 2], in0=q_rest[h][:], in1=q_pieces[:, tiles, 1], op=SUBTRACT)
 
         def rows_of_q(h):
             pieces_turned = psum.tile([P, TILES, P], BF16, tag="bank")
@@ -253,8 +278,9 @@ def tile_cross_module_pa_kernel(tc, x1, wq1, bq1, wv1, bv1, k2, out):
                     start=True,
                     stop=True,
                 )
+            i = chunk_of(m_tile)
             nc.scalar.activation(
-                out=att_grouped[:, g, block(m_tile), :],
+                out=att_grouped[i][:, g, block(m_tile - CHUNKS[i][0]), :],
                 in_=product[:].rearrange("p j m -> p m j"),
                 func=SIGMOID,
                 scale=-1.0,
@@ -283,27 +309,30 @@ def tile_cross_module_pa_kernel(tc, x1, wq1, bq1, wv1, bv1, k2, out):
                 op=ADD,
             )
 
-        def output_pass(sums, columns, c_tile, g):
+        def output_pass(sums, i, c_tile, g):
             nc.tensor.matmul_mx(
                 out=sums[:],
                 lhsT=v_codes[:, c_tile, g, :].bitcast(FP8X4),
                 lhsT_scale=v_scales[:, c_tile, g, :],
-                rhs=att_codes[:, g, columns].bitcast(FP8X4),
-                rhs_scale=att_scales[:, g, columns],
+                rhs=att_codes[i][:, g, :].bitcast(FP8X4),
+                rhs_scale=att_scales[i][:, g, :],
                 start=(g == 0),
                 stop=(g == PASSES - 1),
             )
 
-        def output_bank(columns):
-            return psum.tile([P, columns.stop - columns.start], F32, name="out_sums", tag="bank")
+        def chunk_pixels(i):
+            return slice(CHUNKS[i][0] * P, CHUNKS[i][1] * P)
 
-        def store_output(sums, columns, c_tile, on_scalar):
-            result = ring.tile([P, columns.stop - columns.start], F32, name="result")
+        def output_bank(i):
+            return psum.tile([P, (CHUNKS[i][1] - CHUNKS[i][0]) * P], F32, name="out_sums", tag="bank")
+
+        def store_output(sums, i, c_tile, on_scalar):
+            result = ring.tile([P, (CHUNKS[i][1] - CHUNKS[i][0]) * P], F32, name="result")
             if on_scalar:
                 nc.scalar.copy(out=result[:], in_=sums[:])
             else:
                 nc.vector.tensor_copy(out=result[:], in_=sums[:])
-            nc.sync.dma_start(out=out_rows[block(c_tile), columns], in_=result[:])
+            nc.sync.dma_start(out=out_rows[block(c_tile), chunk_pixels(i)], in_=result[:])
 
         keep_clock(12)
         regroup_x(0, 0, 0, 320, False)
@@ -322,119 +351,110 @@ def tile_cross_module_pa_kernel(tc, x1, wq1, bq1, wv1, bv1, k2, out):
             for g in range(PASSES):
                 project_q(sums0, 0, g, t)
         best = max_first(sums0)
-        regroup_x(0, 1, 192, 512, True)
+        regroup_x(0, 1, 256, 512, True)
         regroup_x(1, 1, 192, 512, True)
         bv_bank = bv_sums()
-        keep_clock(4)
+        keep_clock(2)
         turn(wv_rows, wv_grouped, 0, True)
         turn(wv_rows, wv_grouped, 1, True)
-        keep_clock(2)
-        regroup_x(0, 1, 0, 192, False)
+        regroup_x(0, 1, 0, 256, False)
         best = max_next(sums0, best, 1)
-        regroup_x(1, 1, 0, 192, False)
-        best = max_next(sums0, best, 2)
-        best = max_next(sums0, best, 3)
         quantise_x(0, 1)
-        best_turned = turn_best(best)
-        bv_copy(bv_bank)
+        best = max_next(sums0, best, 2)
         sums1 = banks("q_sums", HALF)
         for t in range(TILES):
             project_q(sums1, 1, 0, t)
+        turn(wv_rows, wv_grouped, 2, True)
+        regroup_x(1, 1, 0, 192, False)
+        best = max_next(sums0, best, 3)
         quantise_x(1, 1)
+        best_turned = turn_best(best)
+        turn(wv_rows, wv_grouped, 3, True)
+        quantise_weight(wv_grouped, wv_codes, wv_scales, 0)
         for t in range(TILES):
             project_q(sums1, 1, 1, t)
         reduce_best(best_turned, 0)
-        quantise_weight(wv_grouped, wv_codes, wv_scales, 0)
         piece_high(0)
         best = max_first(sums1)
+        bv_copy(bv_bank)
         quantise_weight(wv_grouped, wv_codes, wv_scales, 1)
         piece_middle(0)
         piece_low(0)
-        rows_of_q(0)
         v00 = value_sums(0, 0)
-        turn(wv_rows, wv_grouped, 2, True)
+        rows_of_q(0)
         best = max_next(sums1, best, 1)
+        v10 = value_sums(1, 0)
+        v01 = value_sums(0, 1)
         attention_tile(0, 0)
         attention_tile(1, 0)
         best = max_next(sums1, best, 2)
-        chunk1 = slice(512, 768)
-        chunk2 = slice(768, 1024)
         attention_tile(0, 1)
         best = max_next(sums1, best, 3)
         attention_tile(1, 1)
         value_add(v00, 0, 0)
         best_turned = turn_best(best)
-        turn(wv_rows, wv_grouped, 3, True)
-        v10 = value_sums(1, 0)
         attention_tile(0, 2)
         attention_tile(1, 2)
         quantise_weight(wv_grouped, wv_codes, wv_scales, 2)
-        v01 = value_sums(0, 1)
         reduce_best(best_turned, 1)
-        piece_high(1)
-        piece_middle(1)
-        piece_low(1)
+        split_q(1, nc.gpsimd)
+        v11 = value_sums(1, 1)
         attention_tile(0, 3)
         value_add(v10, 1, 0)
-        rows_of_q(1)
         quantise_weight(wv_grouped, wv_codes, wv_scales, 3)
-        v11 = value_sums(1, 1)
         value_add(v01, 0, 1)
-        quantise_v(0)
-        attention_tile(1, 3)
         v02 = value_sums(0, 2)
+        quantise_v(0)
+        v12 = value_sums(1, 2)
+        rows_of_q(1)
         value_add(v11, 1, 1)
-        attention_tile(0, 4)
-        attention_tile(1, 4)
+        attention_tile(1, 3)
         value_add(v02, 0, 2)
         quantise_v(1)
-        v12 = value_sums(1, 2)
-        attention_tile(0, 5)
-        quantise_att(0, half(0))
-        quantise_att(1, half(0))
-        attention_tile(1, 5)
-        value_add(v12, 1, 2)
         v03 = value_sums(0, 3)
-        attention_tile(0, 6)
-        out00 = output_bank(half(0))
-        output_pass(out00, half(0), 0, 0)
-        output_pass(out00, half(0), 0, 1)
-        value_add(v03, 0, 3)
+        attention_tile(0, 4)
+        attention_tile(1, 4)
+        value_add(v12, 1, 2)
         quantise_v(2)
-        attention_tile(0, 7)
+        attention_tile(0, 5)
         v13 = value_sums(1, 3)
-        store_output(out00, half(0), 0, False)
-        attention_tile(1, 6)
-        out01 = output_bank(half(0))
-        output_pass(out01, half(0), 1, 0)
-        output_pass(out01, half(0), 1, 1)
+        quantise_att(0)
+        value_add(v03, 0, 3)
+        attention_tile(1, 5)
+        attention_tile(0, 6)
+        attention_tile(0, 7)
         value_add(v13, 1, 3)
-        attention_tile(1, 7)
-        quantise_att(0, chunk1)
+        out00 = output_bank(0)
+        output_pass(out00, 0, 0, 0)
+        output_pass(out00, 0, 0, 1)
+        store_output(out00, 0, 0, False)
+        attention_tile(1, 6)
+        out01 = output_bank(0)
+        output_pass(out01, 0, 1, 0)
+        output_pass(out01, 0, 1, 1)
         quantise_v(3)
-        store_output(out01, half(0), 1, False)
-        out02 = output_bank(half(0))
-        output_pass(out02, half(0), 2, 0)
-        output_pass(out02, half(0), 2, 1)
-        quantise_att(1, chunk1)
-        out03 = output_bank(half(0))
-        output_pass(out03, half(0), 3, 0)
-        output_pass(out03, half(0), 3, 1)
-        store_output(out02, half(0), 2, True)
-        quantise_att(0, chunk2)
+        store_output(out01, 0, 1, False)
+        attention_tile(1, 7)
+        out02 = output_bank(0)
+        output_pass(out02, 0, 2, 0)
+        output_pass(out02, 0, 2, 1)
+        quantise_att(1)
+        out03 = output_bank(0)
+        output_pass(out03, 0, 3, 0)
+        output_pass(out03, 0, 3, 1)
+        store_output(out02, 0, 2, True)
         out1 = []
         for c_tile in range(TILES):
-            out1.append(output_bank(chunk1))
+            out1.append(output_bank(1))
             for g in range(PASSES):
-                output_pass(out1[c_tile], chunk1, c_tile, g)
-        quantise_att(1, chunk2)
-        store_output(out03, half(0), 3, True)
+                output_pass(out1[c_tile], 1, c_tile, g)
+        store_output(out03, 0, 3, True)
+        quantise_att(2)
         out2 = []
         for c_tile in range(TILES):
-            store_output(out1[c_tile], chunk1, c_tile, c_tile % 2 == 1)
+            store_output(out1[c_tile], 1, c_tile, c_tile % 2 == 0)
         for c_tile in range(TILES):
-            out2.append(output_bank(chunk2))
-            output_pass(out2[c_tile], chunk2, c_tile, 0)
-        for c_tile in range(TILES):
-            output_pass(out2[c_tile], chunk2, c_tile, 1)
-            store_output(out2[c_tile], chunk2, c_tile, c_tile % 2 == 0)
+            out2.append(output_bank(2))
+            for g in range(PASSES):
+                output_pass(out2[c_tile], 2, c_tile, g)
+            store_output(out2[c_tile], 2, c_tile, c_tile % 2 == 0)

@@ -59,6 +59,11 @@ def tile_cross_module_pa_kernel(tc, x1, wq1, bq1, wv1, bv1, k2, out):
         load_x(1, 0)
         warm_in = keep.tile([P, 1], F32)
         nc.vector.memset(warm_in[:], 0.0)
+        idle_values = keep.tile([P, 2 * P * PACK], BF16, align_bytes=64)
+        nc.vector.memset(idle_values[:].bitcast(F32), 0.0)
+        idle_codes = keep.tile([P, 2 * P], U32, align_bytes=64)
+        idle_scales = keep.tile([P, 2 * P], U8, align_bytes=64)
+        nc.vector.quantize_mx(out=idle_codes[:].bitcast(FP8X4), scales=idle_scales[:], in_=idle_values[:])
         warm_out = keep.tile([P, 1], F32)
         nc.scalar.activation(out=warm_out[:], in_=warm_in[:], func=SIGMOID)
         bq_cols = keep.tile([P, TILES], BF16)
@@ -80,11 +85,6 @@ def tile_cross_module_pa_kernel(tc, x1, wq1, bq1, wv1, bv1, k2, out):
         for t in range(0, TILES, 2):
             nc.sync.dma_start(out=wv_rows[:, t : t + 2, :], in_=wv_view[:, t : t + 2, :])
 
-        idle_values = keep.tile([P, 2 * P * PACK], BF16, align_bytes=64)
-        nc.vector.memset(idle_values[:].bitcast(F32), 0.0)
-        idle_codes = keep.tile([P, 2 * P], U32, align_bytes=64)
-        idle_scales = keep.tile([P, 2 * P], U8, align_bytes=64)
-        nc.vector.quantize_mx(out=idle_codes[:].bitcast(FP8X4), scales=idle_scales[:], in_=idle_values[:])
         ident_f32 = keep.tile([P, P], F32)
         make_identity(nc, ident_f32[:])
         ident_bf16 = keep.tile([P, P], BF16)
@@ -334,7 +334,7 @@ def tile_cross_module_pa_kernel(tc, x1, wq1, bq1, wv1, bv1, k2, out):
                 nc.vector.tensor_copy(out=result[:], in_=sums[:])
             nc.sync.dma_start(out=out_rows[block(c_tile), chunk_pixels(i)], in_=result[:])
 
-        keep_clock(12)
+        keep_clock(18)
         regroup_x(0, 0, 0, 320, False)
         regroup_x(0, 0, 320, 512, True)
         regroup_x(1, 0, 0, 320, False)
@@ -343,7 +343,9 @@ def tile_cross_module_pa_kernel(tc, x1, wq1, bq1, wv1, bv1, k2, out):
         quantise_x(1, 0)
         for t in range(TILES):
             turn(wq_rows, wq_grouped, t, True)
-            if t < 3:
+            if t == 1:
+                bv_bank = bv_sums()
+            elif t < 3:
                 keep_clock(1)
         sums0 = banks("q_sums", HALF)
         for t in range(TILES):
@@ -352,8 +354,7 @@ def tile_cross_module_pa_kernel(tc, x1, wq1, bq1, wv1, bv1, k2, out):
                 project_q(sums0, 0, g, t)
         best = max_first(sums0)
         regroup_x(0, 1, 256, 512, True)
-        regroup_x(1, 1, 192, 512, True)
-        bv_bank = bv_sums()
+        regroup_x(1, 1, 128, 512, True)
         keep_clock(2)
         turn(wv_rows, wv_grouped, 0, True)
         turn(wv_rows, wv_grouped, 1, True)
@@ -365,7 +366,7 @@ def tile_cross_module_pa_kernel(tc, x1, wq1, bq1, wv1, bv1, k2, out):
         for t in range(TILES):
             project_q(sums1, 1, 0, t)
         turn(wv_rows, wv_grouped, 2, True)
-        regroup_x(1, 1, 0, 192, False)
+        regroup_x(1, 1, 0, 128, False)
         best = max_next(sums0, best, 3)
         quantise_x(1, 1)
         best_turned = turn_best(best)
@@ -415,10 +416,10 @@ def tile_cross_module_pa_kernel(tc, x1, wq1, bq1, wv1, bv1, k2, out):
         attention_tile(0, 4)
         attention_tile(1, 4)
         value_add(v12, 1, 2)
+        quantise_att(0)
         quantise_v(2)
         attention_tile(0, 5)
         v13 = value_sums(1, 3)
-        quantise_att(0)
         value_add(v03, 0, 3)
         attention_tile(1, 5)
         attention_tile(0, 6)

@@ -71,28 +71,37 @@ def tile_cross_module_pa_kernel(tc, x1, wq1, bq1, wv1, bv1, k2, out):
         bv_row = keep.tile([P, OUT_CHANNELS], BF16)
         nc.vector.memset(bv_row[:].bitcast(F32), 0.0)
         nc.scalar.dma_start(out=bv_row[0:1, :], in_=bv1.rearrange("(r c) -> r c", r=1))
-        k2_rows = keep.tile([P, PIXELS], BF16)
-        nc.vector.memset(k2_rows[:].bitcast(F32), 0.0)
-        nc.scalar.dma_start(out=k2_rows[0:4, :], in_=k2.rearrange("b n -> (b n)").partition_broadcast(4))
+        k2_rows = keep.tile([P, TILES, PIXELS], BF16)
+        k2_row = k2.rearrange("b n -> (b n)")
+
+        def load_k2():
+            for t in range(TILES):
+                nc.sync.dma_start(out=k2_rows[4 * t : 4 * t + 4, t, :], in_=k2_row.partition_broadcast(4))
         wq_rows = keep.tile([P, TILES, CHANNELS], BF16)
         wq_view = wq1.rearrange("(p t) c -> p t c", t=TILES)
         for t in range(TILES):
             nc.sync.dma_start(out=wq_rows[:, t, :], in_=wq_view[:, t, :])
-        load_x(0, 1)
-        load_x(1, 1)
         wv_rows = keep.tile([P, TILES, CHANNELS], BF16)
         wv_view = wv1.rearrange("(t p) c -> p t c", p=P)
-        for t in range(0, TILES, 2):
+
+        def load_wv(t):
             nc.sync.dma_start(out=wv_rows[:, t : t + 2, :], in_=wv_view[:, t : t + 2, :])
+
 
         ident_f32 = keep.tile([P, P], F32)
         make_identity(nc, ident_f32[:])
         ident_bf16 = keep.tile([P, P], BF16)
         make_identity(nc, ident_bf16[:])
+        nc.gpsimd.memset(k2_rows[:].rearrange("p t n -> p (t n)").bitcast(F32), 0.0)
+        load_x(0, 1)
+        load_x(1, 1)
+        load_k2()
+        for t in range(0, TILES, 2):
+            load_wv(t)
         ones = keep.tile([P, P], BF16)
         nc.vector.memset(ones[:], 1.0)
-        q_pieces = keep.tile([P, HALVES * TILES, P], BF16)
-        nc.gpsimd.memset(q_pieces[:].rearrange("p t n -> p (t n)").bitcast(F32), 0.0)
+        q_pieces = keep.tile([P, HALVES, P], BF16)
+        nc.gpsimd.memset(q_pieces[:].rearrange("p h n -> p (h n)").bitcast(F32), 0.0)
 
         wq_grouped = keep.tile([P, TILES, PASSES, P, PACK], BF16, align_bytes=64)
         wq_codes = keep.tile([P, TILES, PASSES, P], U32, align_bytes=64)
@@ -119,7 +128,7 @@ def tile_cross_module_pa_kernel(tc, x1, wq1, bq1, wv1, bv1, k2, out):
         q_rest = []
         for h in range(HALVES):
             q_rest.append(keep.tile([P, TILES], F32, name="q_rest_%d" % h))
-        q_rows = keep.tile([P, PIXELS], BF16)
+        q_rows = keep.tile([P, HALVES, P], BF16)
 
         def half(h):
             return slice(h * HALF, (h + 1) * HALF)
@@ -242,39 +251,39 @@ def tile_cross_module_pa_kernel(tc, x1, wq1, bq1, wv1, bv1, k2, out):
         def reduce_best(best_turned, h):
             nc.vector.tensor_reduce(out=q_cols[:, half_tiles(h)], in_=best_turned[:], axis=mybir.AxisListType.X, op=MAX)
 
+        def piece(h, i):
+            return q_pieces[:, h, 0 : 4 * TILES].rearrange("p (t i) -> p t i", i=4)[:, :, i]
+
         def split_q(h, engine):
-            tiles = slice(h * TILES, (h + 1) * TILES)
-            engine.tensor_copy(out=q_pieces[:, tiles, 0], in_=q_cols[:, tiles])
-            engine.tensor_tensor(out=q_rest[h][:], in0=q_cols[:, tiles], in1=q_pieces[:, tiles, 0], op=SUBTRACT)
-            engine.tensor_tensor(out=q_pieces[:, tiles, 1], in0=q_cols[:, tiles], in1=q_pieces[:, tiles, 0], op=SUBTRACT)
-            engine.tensor_tensor(out=q_pieces[:, tiles, 2], in0=q_rest[h][:], in1=q_pieces[:, tiles, 1], op=SUBTRACT)
+            tiles = half_tiles(h)
+            engine.tensor_copy(out=piece(h, 0), in_=q_cols[:, tiles])
+            engine.tensor_tensor(out=q_rest[h][:], in0=q_cols[:, tiles], in1=piece(h, 0), op=SUBTRACT)
+            engine.tensor_tensor(out=piece(h, 1), in0=q_cols[:, tiles], in1=piece(h, 0), op=SUBTRACT)
+            engine.tensor_tensor(out=piece(h, 2), in0=q_rest[h][:], in1=piece(h, 1), op=SUBTRACT)
 
         def piece_high(h):
-            tiles = half_tiles(h)
-            nc.vector.tensor_copy(out=q_pieces[:, tiles, 0], in_=q_cols[:, tiles])
+            nc.vector.tensor_copy(out=piece(h, 0), in_=q_cols[:, half_tiles(h)])
 
         def piece_middle(h):
             tiles = half_tiles(h)
-            nc.vector.tensor_tensor(out=q_rest[h][:], in0=q_cols[:, tiles], in1=q_pieces[:, tiles, 0], op=SUBTRACT)
-            nc.vector.tensor_tensor(out=q_pieces[:, tiles, 1], in0=q_cols[:, tiles], in1=q_pieces[:, tiles, 0], op=SUBTRACT)
+            nc.vector.tensor_tensor(out=q_rest[h][:], in0=q_cols[:, tiles], in1=piece(h, 0), op=SUBTRACT)
+            nc.vector.tensor_tensor(out=piece(h, 1), in0=q_cols[:, tiles], in1=piece(h, 0), op=SUBTRACT)
 
         def piece_low(h):
-            tiles = half_tiles(h)
-            nc.vector.tensor_tensor(out=q_pieces[:, tiles, 2], in0=q_rest[h][:], in1=q_pieces[:, tiles, 1], op=SUBTRACT)
+            nc.vector.tensor_tensor(out=piece(h, 2), in0=q_rest[h][:], in1=piece(h, 1), op=SUBTRACT)
 
         def rows_of_q(h):
-            pieces_turned = psum.tile([P, TILES, P], BF16, tag="bank")
-            for t in range(TILES):
-                nc.tensor.transpose(pieces_turned[:, t, :], q_pieces[:, h * TILES + t, :], ident_bf16[:])
-            nc.scalar.copy(out=q_rows[:, half(h)], in_=pieces_turned[:].rearrange("p t n -> p (t n)"))
+            pieces_turned = psum.tile([P, P], BF16, tag="bank")
+            nc.tensor.matmul(out=pieces_turned[:], lhsT=q_pieces[:, h, :], rhs=ident_bf16[:], start=True, stop=True)
+            nc.scalar.copy(out=q_rows[:, h, :], in_=pieces_turned[:])
 
         def attention_tile(g, m_tile):
             product = psum.tile([P, PACK, P], F32, tag="bank")
             for j in range(PACK):
                 nc.tensor.matmul(
                     out=product[:, j, :],
-                    lhsT=k2_rows[:, block(g * PACK + j)],
-                    rhs=q_rows[:, block(m_tile)],
+                    lhsT=k2_rows[:, m_tile % TILES, block(g * PACK + j)],
+                    rhs=q_rows[:, m_tile // TILES, :],
                     start=True,
                     stop=True,
                 )

@@ -66,11 +66,8 @@ def tile_cross_module_pa_kernel(tc, x1, wq1, bq1, wv1, bv1, k2, out):
         nc.vector.quantize_mx(out=idle_codes[:].bitcast(FP8X4), scales=idle_scales[:], in_=idle_values[:])
         warm_out = keep.tile([P, 1], F32)
         nc.scalar.activation(out=warm_out[:], in_=warm_in[:], func=SIGMOID)
-        bq_cols = keep.tile([P, TILES], BF16)
-        nc.scalar.dma_start(out=bq_cols[:], in_=bq1.rearrange("(p t) -> p t", t=TILES))
         bv_row = keep.tile([P, OUT_CHANNELS], BF16)
         nc.vector.memset(bv_row[:].bitcast(F32), 0.0)
-        nc.scalar.dma_start(out=bv_row[0:1, :], in_=bv1.rearrange("(r c) -> r c", r=1))
         k2_rows = keep.tile([P, TILES, PIXELS], BF16)
         k2_row = k2.rearrange("b n -> (b n)")
 
@@ -81,6 +78,9 @@ def tile_cross_module_pa_kernel(tc, x1, wq1, bq1, wv1, bv1, k2, out):
         wq_view = wq1.rearrange("(p t) c -> p t c", t=TILES)
         for t in range(TILES):
             nc.sync.dma_start(out=wq_rows[:, t, :], in_=wq_view[:, t, :])
+        bq_cols = keep.tile([P, TILES], BF16)
+        nc.sync.dma_start(out=bq_cols[:], in_=bq1.rearrange("(p t) -> p t", t=TILES))
+        nc.sync.dma_start(out=bv_row[0:1, :], in_=bv1.rearrange("(r c) -> r c", r=1))
         wv_rows = keep.tile([P, TILES, CHANNELS], BF16)
         wv_view = wv1.rearrange("(t p) c -> p t c", p=P)
 
@@ -95,9 +95,9 @@ def tile_cross_module_pa_kernel(tc, x1, wq1, bq1, wv1, bv1, k2, out):
         nc.gpsimd.memset(k2_rows[:].rearrange("p t n -> p (t n)").bitcast(F32), 0.0)
         load_x(0, 1)
         load_x(1, 1)
-        load_k2()
         for t in range(0, TILES, 2):
             load_wv(t)
+        load_k2()
         ones = keep.tile([P, P], BF16)
         nc.vector.memset(ones[:], 1.0)
         q_pieces = keep.tile([P, HALVES, P], BF16)
@@ -343,7 +343,7 @@ def tile_cross_module_pa_kernel(tc, x1, wq1, bq1, wv1, bv1, k2, out):
                 nc.vector.tensor_copy(out=result[:], in_=sums[:])
             nc.sync.dma_start(out=out_rows[block(c_tile), chunk_pixels(i)], in_=result[:])
 
-        keep_clock(18)
+        keep_clock(17)
         regroup_x(0, 0, 0, 320, False)
         regroup_x(0, 0, 320, 512, True)
         regroup_x(1, 0, 0, 320, False)
@@ -352,22 +352,19 @@ def tile_cross_module_pa_kernel(tc, x1, wq1, bq1, wv1, bv1, k2, out):
         quantise_x(1, 0)
         for t in range(TILES):
             turn(wq_rows, wq_grouped, t, True)
-            if t == 1:
-                bv_bank = bv_sums()
-            elif t < 3:
-                keep_clock(1)
         sums0 = banks("q_sums", HALF)
         for t in range(TILES):
             quantise_weight(wq_grouped, wq_codes, wq_scales, t)
             for g in range(PASSES):
                 project_q(sums0, 0, g, t)
         best = max_first(sums0)
-        regroup_x(0, 1, 256, 512, True)
+        regroup_x(0, 1, 320, 512, True)
         regroup_x(1, 1, 128, 512, True)
-        keep_clock(2)
+        bv_bank = bv_sums()
         turn(wv_rows, wv_grouped, 0, True)
         turn(wv_rows, wv_grouped, 1, True)
-        regroup_x(0, 1, 0, 256, False)
+        bv_copy(bv_bank)
+        regroup_x(0, 1, 0, 320, False)
         best = max_next(sums0, best, 1)
         quantise_x(0, 1)
         best = max_next(sums0, best, 2)
@@ -386,7 +383,6 @@ def tile_cross_module_pa_kernel(tc, x1, wq1, bq1, wv1, bv1, k2, out):
         reduce_best(best_turned, 0)
         piece_high(0)
         best = max_first(sums1)
-        bv_copy(bv_bank)
         quantise_weight(wv_grouped, wv_codes, wv_scales, 1)
         piece_middle(0)
         piece_low(0)
@@ -406,11 +402,11 @@ def tile_cross_module_pa_kernel(tc, x1, wq1, bq1, wv1, bv1, k2, out):
         attention_tile(0, 2)
         attention_tile(1, 2)
         quantise_weight(wv_grouped, wv_codes, wv_scales, 2)
+        value_add(v10, 1, 0)
         reduce_best(best_turned, 1)
         split_q(1, nc.gpsimd)
         v11 = value_sums(1, 1)
         attention_tile(0, 3)
-        value_add(v10, 1, 0)
         quantise_weight(wv_grouped, wv_codes, wv_scales, 3)
         value_add(v01, 0, 1)
         v02 = value_sums(0, 2)

@@ -343,7 +343,7 @@ def tile_cross_module_pa_kernel(tc, x1, wq1, bq1, wv1, bv1, k2, out):
                 nc.vector.tensor_copy(out=result[:], in_=sums[:])
             nc.sync.dma_start(out=out_rows[block(c_tile), chunk_pixels(i)], in_=result[:])
 
-        keep_clock(17)
+        keep_clock(15)
         regroup_x(0, 0, 0, 320, False)
         regroup_x(0, 0, 320, 512, True)
         regroup_x(1, 0, 0, 320, False)
@@ -405,8 +405,8 @@ def tile_cross_module_pa_kernel(tc, x1, wq1, bq1, wv1, bv1, k2, out):
         value_add(v10, 1, 0)
         reduce_best(best_turned, 1)
         split_q(1, nc.gpsimd)
-        v11 = value_sums(1, 1)
         attention_tile(0, 3)
+        v11 = value_sums(1, 1)
         quantise_weight(wv_grouped, wv_codes, wv_scales, 3)
         value_add(v01, 0, 1)
         v02 = value_sums(0, 2)
@@ -430,11 +430,11 @@ def tile_cross_module_pa_kernel(tc, x1, wq1, bq1, wv1, bv1, k2, out):
         attention_tile(0, 6)
         attention_tile(0, 7)
         value_add(v13, 1, 3)
+        attention_tile(1, 6)
         out00 = output_bank(0)
         output_pass(out00, 0, 0, 0)
         output_pass(out00, 0, 0, 1)
         store_output(out00, 0, 0, False)
-        attention_tile(1, 6)
         out01 = output_bank(0)
         output_pass(out01, 0, 1, 0)
         output_pass(out01, 0, 1, 1)

@@ -254,13 +254,6 @@ def tile_cross_module_pa_kernel(tc, x1, wq1, bq1, wv1, bv1, k2, out):
         def piece(h, i):
             return q_pieces[:, h, 0 : 4 * TILES].rearrange("p (t i) -> p t i", i=4)[:, :, i]
 
-        def split_q(h, engine):
-            tiles = half_tiles(h)
-            engine.tensor_copy(out=piece(h, 0), in_=q_cols[:, tiles])
-            engine.tensor_tensor(out=q_rest[h][:], in0=q_cols[:, tiles], in1=piece(h, 0), op=SUBTRACT)
-            engine.tensor_tensor(out=piece(h, 1), in0=q_cols[:, tiles], in1=piece(h, 0), op=SUBTRACT)
-            engine.tensor_tensor(out=piece(h, 2), in0=q_rest[h][:], in1=piece(h, 1), op=SUBTRACT)
-
         def piece_high(h):
             nc.vector.tensor_copy(out=piece(h, 0), in_=q_cols[:, half_tiles(h)])
 
@@ -404,13 +397,15 @@ def tile_cross_module_pa_kernel(tc, x1, wq1, bq1, wv1, bv1, k2, out):
         quantise_weight(wv_grouped, wv_codes, wv_scales, 2)
         value_add(v10, 1, 0)
         reduce_best(best_turned, 1)
-        split_q(1, nc.gpsimd)
         attention_tile(0, 3)
         v11 = value_sums(1, 1)
         quantise_weight(wv_grouped, wv_codes, wv_scales, 3)
-        value_add(v01, 0, 1)
-        v02 = value_sums(0, 2)
+        piece_high(1)
         quantise_v(0)
+        piece_middle(1)
+        value_add(v01, 0, 1)
+        piece_low(1)
+        v02 = value_sums(0, 2)
         v12 = value_sums(1, 2)
         rows_of_q(1)
         value_add(v11, 1, 1)

from contextlib import ExitStack

import concourse.mybir as mybir
from concourse.masks import make_identity

F32 = mybir.dt.float32
BF16 = mybir.dt.bfloat16
U32 = mybir.dt.uint32
U8 = mybir.dt.uint8
FP8X4 = mybir.dt.float8_e4m3fn_x4
ADD = mybir.AluOpType.add
SUBTRACT = mybir.AluOpType.subtract
MAX = mybir.AluOpType.max
IDENTITY = mybir.ActivationFunctionType.Identity
SIGMOID = mybir.ActivationFunctionType.Sigmoid

P = 128
PACK = 4
K_PASS = P * PACK
CHANNELS = 1024
PIXELS = 1024
OUT_CHANNELS = 512
PASSES = 2
HALF = 512
HALVES = PIXELS // HALF
TILES = OUT_CHANNELS // P
CHUNKS = ((0, 4), (4, 6), (6, 8))
PIECES = 3

FLOPS = 3 * 2 * OUT_CHANNELS * CHANNELS * PIXELS


def tile_cross_module_pa_kernel(tc, x1, wq1, bq1, wv1, bv1, k2, out):
    nc = tc.nc
    x_rows = x1.rearrange("b c h w -> (b c) (h w)")
    out_rows = out.rearrange("b c h w -> (b c) (h w)")

    with ExitStack() as ctx:
        keep = ctx.enter_context(tc.tile_pool(name="keep", bufs=1))
        ring = ctx.enter_context(tc.tile_pool(name="ring", bufs=12))
        psum = ctx.enter_context(tc.psum_pool(name="psum", bufs=8))
        ctx.enter_context(tc.manual_schedule())

        x_raw = []
        for g in range(PASSES):
            x_raw.append([])
            for h in range(HALVES):
                x_raw[g].append(keep.tile([P, PACK, HALF], BF16, name="x_raw_%d_%d" % (g, h)))

        def load_x(g, h):
            for u in range(2):
                first = g * K_PASS + u * 2 * P
                nc.sync.dma_start(
                    out=x_raw[g][h][:, 2 * u : 2 * u + 2, :],
                    in_=x_rows[first : first + 2 * P, h * HALF : (h + 1) * HALF].rearrange("(q e) n -> q e n", e=2),
                )

        load_x(0, 0)
        load_x(1, 0)
        warm_in = keep.tile([P, 1], F32)
        nc.vector.memset(warm_in[:], 0.0)
        idle_values = keep.tile([P, 2 * P * PACK], BF16, align_bytes=64)
        nc.vector.memset(idle_values[:].bitcast(F32), 0.0)
        idle_codes = keep.tile([P, 2 * P], U32, align_bytes=64)
        idle_scales = keep.tile([P, 2 * P], U8, align_bytes=64)
        nc.vector.quantize_mx(out=idle_codes[:].bitcast(FP8X4), scales=idle_scales[:], in_=idle_values[:])
        warm_out = keep.tile([P, 1], F32)
        nc.scalar.activation(out=warm_out[:], in_=warm_in[:], func=SIGMOID)
        bv_row = keep.tile([P, OUT_CHANNELS], BF16)
        nc.vector.memset(bv_row[:].bitcast(F32), 0.0)
        k2_rows = keep.tile([P, TILES, PIXELS], BF16)
        k2_row = k2.rearrange("b n -> (b n)")

        def load_k2():
            for t in range(TILES):
                nc.sync.dma_start(out=k2_rows[4 * t : 4 * t + 4, t, :], in_=k2_row.partition_broadcast(4))
        wq_rows = keep.tile([P, TILES, CHANNELS], BF16)
        wq_view = wq1.rearrange("(p t) c -> p t c", t=TILES)
        for t in range(TILES):
            nc.sync.dma_start(out=wq_rows[:, t, :], in_=wq_view[:, t, :])
        bq_cols = keep.tile([P, TILES], BF16)
        nc.sync.dma_start(out=bq_cols[:], in_=bq1.rearrange("(p t) -> p t", t=TILES))
        nc.sync.dma_start(out=bv_row[0:1, :], in_=bv1.rearrange("(r c) -> r c", r=1))
        wv_rows = keep.tile([P, TILES, CHANNELS], BF16)
        wv_view = wv1.rearrange("(t p) c -> p t c", p=P)

        def load_wv(t):
            nc.sync.dma_start(out=wv_rows[:, t : t + 2, :], in_=wv_view[:, t : t + 2, :])


        ident_f32 = keep.tile([P, P], F32)
        make_identity(nc, ident_f32[:])
        ident_bf16 = keep.tile([P, P], BF16)
        make_identity(nc, ident_bf16[:])
        nc.gpsimd.memset(k2_rows[:].rearrange("p t n -> p (t n)").bitcast(F32), 0.0)
        load_x(0, 1)
        load_x(1, 1)
        for t in range(0, TILES, 2):
            load_wv(t)
        load_k2()
        ones = keep.tile([P, P], BF16)
        nc.vector.memset(ones[:], 1.0)
        q_pieces = keep.tile([P, HALVES, P], BF16)
        nc.gpsimd.memset(q_pieces[:].rearrange("p h n -> p (h n)").bitcast(F32), 0.0)

        wq_grouped = keep.tile([P, TILES, PASSES, P, PACK], BF16, align_bytes=64)
        wq_codes = keep.tile([P, TILES, PASSES, P], U32, align_bytes=64)
        wq_scales = keep.tile([P, TILES, PASSES, P], U8, align_bytes=64)
        wv_grouped = keep.tile([P, TILES, PASSES, P, PACK], BF16, align_bytes=64)
        wv_codes = keep.tile([P, TILES, PASSES, P], U32, align_bytes=64)
        wv_scales = keep.tile([P, TILES, PASSES, P], U8, align_bytes=64)
        x_grouped = keep.tile([P, PASSES, PIXELS, PACK], BF16, align_bytes=64)
        x_codes = keep.tile([P, PASSES, PIXELS], U32, align_bytes=64)
        x_scales = keep.tile([P, PASSES, PIXELS], U8, align_bytes=64)
        att_grouped = []
        att_codes = []
        att_scales = []
        for i in range(len(CHUNKS)):
            width = (CHUNKS[i][1] - CHUNKS[i][0]) * P
            att_grouped.append(keep.tile([P, PASSES, width, PACK], BF16, name="att_grouped_%d" % i, align_bytes=64))
            att_codes.append(keep.tile([P, PASSES, width], U32, name="att_codes_%d" % i, align_bytes=64))
            att_scales.append(keep.tile([P, PASSES, width], U8, name="att_scales_%d" % i, align_bytes=64))
        v_grouped = keep.tile([P, TILES, PASSES, P, PACK], BF16, align_bytes=64)
        v_codes = keep.tile([P, TILES, PASSES, P], U32, align_bytes=64)
        v_scales = keep.tile([P, TILES, PASSES, P], U8, align_bytes=64)
        bv_all = keep.tile([P, OUT_CHANNELS], F32)
        q_cols = keep.tile([P, HALVES * TILES], F32)
        q_rest = []
        for h in range(HALVES):
            q_rest.append(keep.tile([P, TILES], F32, name="q_rest_%d" % h))
        q_rows = keep.tile([P, HALVES, P], BF16)

        def half(h):
            return slice(h * HALF, (h + 1) * HALF)

        def block(t):
            return slice(t * P, (t + 1) * P)

        def turn(rows, grouped, t, on_scalar):
            words = rows[:, t, :].bitcast(F32)
            turned = psum.tile([P, PASSES * 2, P], F32, name="turned", tag="bank")
            for b in range(PASSES * 2):
                nc.tensor.transpose(turned[:, b, :], words[:, block(b)], ident_f32[:])
            grouped_words = grouped[:, t].rearrange("p g o k -> p (g o k)").bitcast(F32).rearrange("p (g o u) -> p g o u", g=PASSES, u=2)
            turned_words = turned[:].rearrange("p (g u) o -> p g o u", u=2)
            if on_scalar:
                nc.scalar.copy(out=grouped_words, in_=turned_words)
            else:
                nc.vector.tensor_copy(out=grouped_words, in_=turned_words)

        def quantise_weight(grouped, codes, scales, t):
            nc.vector.quantize_mx(
                out=codes[:, t].rearrange("p g o -> p (g o)").bitcast(FP8X4),
                scales=scales[:, t].rearrange("p g o -> p (g o)"),
                in_=grouped[:, t].rearrange("p g o k -> p (g o k)"),
            )

        def keep_clock(passes):
            idle_bank = psum.tile([P, PASSES * P], F32, tag="bank")
            for step in range(passes):
                nc.tensor.matmul_mx(
                    out=idle_bank[:],
                    lhsT=idle_codes[:, 0:P].bitcast(FP8X4),
                    lhsT_scale=idle_scales[:, 0:P],
                    rhs=idle_codes[:].bitcast(FP8X4),
                    rhs_scale=idle_scales[:],
                    start=True,
                    stop=True,
                )

        def bv_sums():
            bv_bank = psum.tile([P, OUT_CHANNELS], F32, tag="bank")
            nc.tensor.matmul(out=bv_bank[:], lhsT=ones[:], rhs=bv_row[:], start=True, stop=True)
            return bv_bank

        def bv_copy(bv_bank):
            nc.scalar.copy(out=bv_all[:], in_=bv_bank[:])

        def regroup_x(g, h, first, last, on_scalar):
            start = h * HALF
            regrouped = x_grouped[:, g, start + first : start + last, :].rearrange("p (n i) t -> p n t i", i=4)
            as_loaded = x_raw[g][h][:, :, first:last].rearrange("p t (n i) -> p n t i", i=4)
            if on_scalar:
                nc.scalar.copy(out=regrouped, in_=as_loaded)
            else:
                nc.vector.tensor_copy(out=regrouped, in_=as_loaded)

        def quantise_columns(grouped, codes, scales, g, columns):
            nc.vector.quantize_mx(
                out=codes[:, g, columns].bitcast(FP8X4),
                scales=scales[:, g, columns],
                in_=grouped[:, g, columns, :].rearrange("p n t -> p (n t)"),
            )

        def quantise_x(g, h):
            quantise_columns(x_grouped, x_codes, x_scales, g, half(h))

        def quantise_v(c_tile):
            quantise_weight(v_grouped, v_codes, v_scales, c_tile)

        def quantise_att(i):
            nc.vector.quantize_mx(
                out=att_codes[i][:].rearrange("p g m -> p (g m)").bitcast(FP8X4),
                scales=att_scales[i][:].rearrange("p g m -> p (g m)"),
                in_=att_grouped[i][:].rearrange("p g m k -> p (g m k)"),
            )

        def chunk_of(m_tile):
            for i in range(len(CHUNKS)):
                if m_tile < CHUNKS[i][1]:
                    return i

        def project_q(sums, h, g, t):
            nc.tensor.matmul_mx(
                out=sums[t][:],
                lhsT=wq_codes[:, t, g, :].bitcast(FP8X4),
                lhsT_scale=wq_scales[:, t, g, :],
                rhs=x_codes[:, g, half(h)].bitcast(FP8X4),
                rhs_scale=x_scales[:, g, half(h)],
                start=(g == 0),
                stop=(g == PASSES - 1),
            )

        def banks(label, width):
            made = []
            for t in range(TILES):
                made.append(psum.tile([P, width], F32, name=label, tag="bank"))
            return made

        def max_first(sums):
            best = ring.tile([P, HALF], F32, name="best")
            nc.scalar.activation(out=best[:], in_=sums[0][:], func=IDENTITY, bias=bq_cols[:, 0:1])
            return best

        def max_next(sums, best, t):
            better = ring.tile([P, HALF], F32, name="best")
            nc.vector.scalar_tensor_tensor(
                out=better[:], in0=sums[t][:], scalar=bq_cols[:, t : t + 1], in1=best[:], op0=ADD, op1=MAX
            )
            return better

        def turn_best(best):
            best_turned = psum.tile([P, TILES, P], F32, tag="bank")
            for t in range(TILES):
                nc.tensor.transpose(best_turned[:, t, :], best[:, block(t)], ident_f32[:])
            return best_turned

        def half_tiles(h):
            return slice(h * TILES, (h + 1) * TILES)

        def reduce_best(best_turned, h):
            nc.vector.tensor_reduce(out=q_cols[:, half_tiles(h)], in_=best_turned[:], axis=mybir.AxisListType.X, op=MAX)

        def piece(h, i):
            return q_pieces[:, h, 0 : 4 * TILES].rearrange("p (t i) -> p t i", i=4)[:, :, i]

        def piece_high(h):
            nc.vector.tensor_copy(out=piece(h, 0), in_=q_cols[:, half_tiles(h)])

        def piece_middle(h):
            tiles = half_tiles(h)
            nc.vector.tensor_tensor(out=q_rest[h][:], in0=q_cols[:, tiles], in1=piece(h, 0), op=SUBTRACT)
            nc.vector.tensor_tensor(out=piece(h, 1), in0=q_cols[:, tiles], in1=piece(h, 0), op=SUBTRACT)

        def piece_low(h):
            nc.vector.tensor_tensor(out=piece(h, 2), in0=q_rest[h][:], in1=piece(h, 1), op=SUBTRACT)

        def rows_of_q(h):
            pieces_turned = psum.tile([P, P], BF16, tag="bank")
            nc.tensor.matmul(out=pieces_turned[:], lhsT=q_pieces[:, h, :], rhs=ident_bf16[:], start=True, stop=True)
            nc.scalar.copy(out=q_rows[:, h, :], in_=pieces_turned[:])

        def attention_tile(g, m_tile):
            product = psum.tile([P, PACK, P], F32, tag="bank")
            for j in range(PACK):
                nc.tensor.matmul(
                    out=product[:, j, :],
                    lhsT=k2_rows[:, m_tile % TILES, block(g * PACK + j)],
                    rhs=q_rows[:, m_tile // TILES, :],
                    start=True,
                    stop=True,
                )
            i = chunk_of(m_tile)
            nc.scalar.activation(
                out=att_grouped[i][:, g, block(m_tile - CHUNKS[i][0]), :],
                in_=product[:].rearrange("p j m -> p m j"),
                func=SIGMOID,
                scale=-1.0,
            )

        def value_sums(g, c_tile):
            sums = psum.tile([P, PACK, P], F32, name="v_sums", tag="bank")
            for j in range(PACK):
                for gc in range(PASSES):
                    nc.tensor.matmul_mx(
                        out=sums[:, j, :],
                        lhsT=x_codes[:, gc, block(g * PACK + j)].bitcast(FP8X4),
                        lhsT_scale=x_scales[:, gc, block(g * PACK + j)],
                        rhs=wv_codes[:, c_tile, gc, :].bitcast(FP8X4),
                        rhs_scale=wv_scales[:, c_tile, gc, :],
                        start=(gc == 0),
                        stop=(gc == PASSES - 1),
                    )
            return sums

        def value_add(sums, g, c_tile):
            nc.vector.tensor_tensor(
                out=v_grouped[:, c_tile, g],
                in0=sums[:].rearrange("p j c -> p c j"),
                in1=bv_all[:, block(c_tile)].unsqueeze(2).to_broadcast([P, P, PACK]),
                op=ADD,
            )

        def output_pass(sums, i, c_tile, g):
            nc.tensor.matmul_mx(
                out=sums[:],
                lhsT=v_codes[:, c_tile, g, :].bitcast(FP8X4),
                lhsT_scale=v_scales[:, c_tile, g, :],
                rhs=att_codes[i][:, g, :].bitcast(FP8X4),
                rhs_scale=att_scales[i][:, g, :],
                start=(g == 0),
                stop=(g == PASSES - 1),
            )

        def chunk_pixels(i):
            return slice(CHUNKS[i][0] * P, CHUNKS[i][1] * P)

        def output_bank(i):
            return psum.tile([P, (CHUNKS[i][1] - CHUNKS[i][0]) * P], F32, name="out_sums", tag="bank")

        def store_output(sums, i, c_tile, on_scalar):
            result = ring.tile([P, (CHUNKS[i][1] - CHUNKS[i][0]) * P], F32, name="result")
            if on_scalar:
                nc.scalar.copy(out=result[:], in_=sums[:])
            else:
                nc.vector.tensor_copy(out=result[:], in_=sums[:])
            nc.sync.dma_start(out=out_rows[block(c_tile), chunk_pixels(i)], in_=result[:])

        keep_clock(15)
        regroup_x(0, 0, 0, 320, False)
        regroup_x(0, 0, 320, 512, True)
        regroup_x(1, 0, 0, 320, False)
        regroup_x(1, 0, 320, 512, True)
        quantise_x(0, 0)
        quantise_x(1, 0)
        for t in range(TILES):
            turn(wq_rows, wq_grouped, t, True)
        sums0 = banks("q_sums", HALF)
        for t in range(TILES):
            quantise_weight(wq_grouped, wq_codes, wq_scales, t)
            for g in range(PASSES):
                project_q(sums0, 0, g, t)
        best = max_first(sums0)
        regroup_x(0, 1, 320, 512, True)
        regroup_x(1, 1, 128, 512, True)
        bv_bank = bv_sums()
        turn(wv_rows, wv_grouped, 0, True)
        turn(wv_rows, wv_grouped, 1, True)
        bv_copy(bv_bank)
        regroup_x(0, 1, 0, 320, False)
        best = max_next(sums0, best, 1)
        quantise_x(0, 1)
        best = max_next(sums0, best, 2)
        sums1 = banks("q_sums", HALF)
        for t in range(TILES):
            project_q(sums1, 1, 0, t)
        turn(wv_rows, wv_grouped, 2, True)
        regroup_x(1, 1, 0, 128, False)
        best = max_next(sums0, best, 3)
        quantise_x(1, 1)
        best_turned = turn_best(best)
        turn(wv_rows, wv_grouped, 3, True)
        quantise_weight(wv_grouped, wv_codes, wv_scales, 0)
        for t in range(TILES):
            project_q(sums1, 1, 1, t)
        reduce_best(best_turned, 0)
        piece_high(0)
        best = max_first(sums1)
        quantise_weight(wv_grouped, wv_codes, wv_scales, 1)
        piece_middle(0)
        piece_low(0)
        v00 = value_sums(0, 0)
        rows_of_q(0)
        best = max_next(sums1, best, 1)
        v10 = value_sums(1, 0)
        v01 = value_sums(0, 1)
        attention_tile(0, 0)
        attention_tile(1, 0)
        best = max_next(sums1, best, 2)
        attention_tile(0, 1)
        best = max_next(sums1, best, 3)
        attention_tile(1, 1)
        value_add(v00, 0, 0)
        best_turned = turn_best(best)
        attention_tile(0, 2)
        attention_tile(1, 2)
        quantise_weight(wv_grouped, wv_codes, wv_scales, 2)
        value_add(v10, 1, 0)
        reduce_best(best_turned, 1)
        attention_tile(0, 3)
        v11 = value_sums(1, 1)
        quantise_weight(wv_grouped, wv_codes, wv_scales, 3)
        piece_high(1)
        quantise_v(0)
        piece_middle(1)
        value_add(v01, 0, 1)
        piece_low(1)
        v02 = value_sums(0, 2)
        v12 = value_sums(1, 2)
        rows_of_q(1)
        value_add(v11, 1, 1)
        attention_tile(1, 3)
        value_add(v02, 0, 2)
        quantise_v(1)
        v03 = value_sums(0, 3)
        attention_tile(0, 4)
        attention_tile(1, 4)
        value_add(v12, 1, 2)
        quantise_att(0)
        quantise_v(2)
        attention_tile(0, 5)
        v13 = value_sums(1, 3)
        value_add(v03, 0, 3)
        attention_tile(1, 5)
        attention_tile(0, 6)
        attention_tile(0, 7)
        value_add(v13, 1, 3)
        attention_tile(1, 6)
        out00 = output_bank(0)
        output_pass(out00, 0, 0, 0)
        output_pass(out00, 0, 0, 1)
        store_output(out00, 0, 0, False)
        out01 = output_bank(0)
        output_pass(out01, 0, 1, 0)
        output_pass(out01, 0, 1, 1)
        quantise_v(3)
        store_output(out01, 0, 1, False)
        attention_tile(1, 7)
        out02 = output_bank(0)
        output_pass(out02, 0, 2, 0)
        output_pass(out02, 0, 2, 1)
        quantise_att(1)
        out03 = output_bank(0)
        output_pass(out03, 0, 3, 0)
        output_pass(out03, 0, 3, 1)
        store_output(out02, 0, 2, True)
        out1 = []
        for c_tile in range(TILES):
            out1.append(output_bank(1))
            for g in range(PASSES):
                output_pass(out1[c_tile], 1, c_tile, g)
        store_output(out03, 0, 3, True)
        quantise_att(2)
        out2 = []
        for c_tile in range(TILES):
            store_output(out1[c_tile], 1, c_tile, c_tile % 2 == 0)
        for c_tile in range(TILES):
            out2.append(output_bank(2))
            for g in range(PASSES):
                output_pass(out2[c_tile], 2, c_tile, g)
            store_output(out2[c_tile], 2, c_tile, c_tile % 2 == 0)
